import numpy as np
import ml_dtypes


def mxq(x, axis, fmt="e4m3"):
    dtype, down = {"e4m3": (ml_dtypes.float8_e4m3fn, 7), "e5m2": (ml_dtypes.float8_e5m2, 14)}[fmt]
    v = np.moveaxis(np.asarray(x, np.float32).astype(ml_dtypes.bfloat16).astype(np.float64), axis, -1)
    blocks = v.reshape(v.shape[:-1] + (-1, 32))
    amax = np.abs(blocks).max(-1, keepdims=True)
    byte = np.maximum(np.where(amax > 0, np.frexp(amax)[1] - 1 + 127, 0) - down, 1)
    scale = np.exp2(byte - 127.0)
    codes = (blocks / scale).astype(np.float32).astype(dtype).astype(np.float64)
    return np.moveaxis((codes * scale).reshape(v.shape), -1, axis)


WIDE = False


def mx_kscale(k):
    if not WIDE:
        return np.ones(k)
    levels = np.array([10, -10, 5, -5, 0])
    a = np.random.permutation(np.resize(levels, k // 512 * 4)).reshape(k // 512, 4)
    idx = np.arange(k)
    return np.exp2(a[idx // 512, idx % 128 // 32])


BF16 = ml_dtypes.bfloat16


def bf(x):
    return np.asarray(x, np.float32).astype(BF16)


def f64(x):
    return np.asarray(x).astype(np.float64)


E2M1 = np.array([0.0, 0.5, 1.0, 1.5, 2.0, 3.0, 4.0, 6.0, -0.0, -0.5, -1.0, -1.5, -2.0, -3.0, -4.0, -6.0])


def pack_weight(w, fmt):
    k, n = w.shape
    w = f64(bf(w)).reshape(k // 32, 32, n)
    amax = np.abs(w).max(1)
    if fmt == "e4m3":
        byte = np.frexp(amax)[1] - 1 + 127 - 7
    else:
        mant, ex = np.frexp(amax / 6.0)
        byte = np.where(mant > 0.5, ex, ex - 1) + 127
    byte = np.clip(np.where(amax > 0, byte, 1), 1, 254)
    scaled = (w * np.exp2(127.0 - byte)[:, None, :]).reshape(k, n).astype(np.float32)
    by_word = np.ascontiguousarray(scaled.reshape(k // 512, 128, 4, n).transpose(0, 1, 3, 2))
    if fmt == "e4m3":
        words = by_word.astype(ml_dtypes.float8_e4m3fn).view(np.uint8)
    else:
        c = by_word.astype(ml_dtypes.float4_e2m1fn).view(np.uint8) & 0xF
        words = c[..., 0::2] | (c[..., 1::2] << 4)
    return np.ascontiguousarray(words), np.ascontiguousarray(byte.astype(np.uint8).reshape(k // 512, 16, n))


def unpack_weight(words, scales, fmt):
    g, p, n, _ = words.shape
    if fmt == "e4m3":
        vals = np.ascontiguousarray(words).view(ml_dtypes.float8_e4m3fn).astype(np.float64)
    else:
        nib = np.empty((g, p, n, 4), np.uint8)
        nib[..., 0::2] = words & 0xF
        nib[..., 1::2] = words >> 4
        vals = E2M1[nib]
    vals = vals * np.repeat(np.exp2(scales.astype(np.float64) - 127.0), 8, axis=1)[..., None]
    return vals.transpose(0, 1, 3, 2).reshape(g * 512, n)


BS, BLOCK, HID, GAP, G = 4096, 512, 512, 64, 2


def elu(v):
    return np.where(v > 0.0, v, np.exp(np.minimum(v, 0.0)) - 1.0)


def setup_inputs():
    s = mx_kscale(BLOCK)
    s = s / s.max()
    y_lanes = bf((np.random.standard_normal((BS, BLOCK, G)) * 1.3 * s[None, :, None]).reshape(BS, BLOCK * G))
    w1 = np.random.standard_normal((G, BLOCK, HID)) / np.sqrt(BLOCK) / s[None, :, None]
    b1 = bf(np.random.standard_normal((G, 1, HID)) * 0.2)
    w2 = np.random.standard_normal((G, HID, BLOCK)) / np.sqrt(HID)
    b2 = bf(np.random.standard_normal((G, 1, BLOCK)) * 0.2)
    w1_words, w1_scales = pack_weight(w1.reshape(-1, HID), "e4m3")
    w2_words, w2_scales = pack_weight(w2.reshape(-1, BLOCK), "e4m3")
    return {"y_lanes": y_lanes,
            "w1_words": w1_words,
            "w1_scales": w1_scales,
            "b1": b1,
            "w2_words": w2_words,
            "w2_scales": w2_scales,
            "b2": b2}


def reference(y_lanes, w1_words, w1_scales, b1, w2_words, w2_scales, b2):
    y = f64(y_lanes)
    bs = y.shape[0]
    y = y.reshape(-1, BLOCK, G).transpose(0, 2, 1).reshape(bs, -1)
    z = y.reshape(bs, -1, BLOCK).transpose(1, 0, 2)
    h = elu((mxq(z, 2, "e4m3") @ unpack_weight(w1_words, w1_scales, "e4m3").reshape(G, BLOCK, HID)) + f64(b1))
    h = (mxq(h, 2, "e4m3") @ unpack_weight(w2_words, w2_scales, "e4m3").reshape(G, HID, BLOCK)) + f64(b2)
    z = h + z
    y = z.transpose(1, 0, 2).reshape(bs, -1)
    return y.reshape(-1, G, BLOCK).transpose(0, 2, 1).reshape(bs, -1)

@@ -1,0 +1,249 @@
+import concourse.mybir as mybir
+from concourse.masks import make_identity
+
+F32 = mybir.dt.float32
+BF16 = mybir.dt.bfloat16
+I32 = mybir.dt.int32
+U32 = mybir.dt.uint32
+U8 = mybir.dt.uint8
+FP8X4 = mybir.dt.float8_e4m3fn_x4
+ACT = mybir.ActivationFunctionType
+ALU = mybir.AluOpType
+
+P = 128
+PACK = 4
+LANES = 2
+ROWS = 4096
+FEAT = 512
+HALF = FEAT // 2
+N_TILES = ROWS // P
+CHUNK = 4
+LAST_STAGE = 4
+
+FLOPS = 2 * 2 * LANES * ROWS * FEAT * FEAT
+
+
+def load_weight(nc, pool, words, scales, label):
+    codes = pool.tile([P, LANES, FEAT], U32, name=label + "_codes", align_bytes=64)
+    plane = pool.tile([P, LANES, FEAT], U8, name=label + "_plane", align_bytes=64)
+    nc.vector.memset(plane[:].bitcast(I32), 0)
+    nc.sync.dma_start(
+        out=codes[:].bitcast(I32),
+        in_=words.rearrange("g p n t -> p g (n t)").bitcast(I32),
+    )
+    for quadrant in range(4):
+        nc.sync.dma_start(
+            out=plane[32 * quadrant : 32 * quadrant + 4, :, :].bitcast(I32),
+            in_=scales[:, 4 * quadrant : 4 * quadrant + 4, :].bitcast(I32).rearrange("g r n -> r g n"),
+        )
+    return codes, plane
+
+
+def tile_blockresmlp_mixerblock_pa_t_e_kernel(
+    tc, y_lanes, w1_words, w1_scales, b1, w2_words, w2_scales, b2, out
+):
+    nc = tc.nc
+    y_rows = y_lanes.rearrange("(p k) c -> p k c", k=N_TILES)
+    out_rows = out.rearrange("(p k) c -> p k c", k=N_TILES)
+
+    with (
+        tc.tile_pool(name="const", bufs=1) as const,
+        tc.tile_pool(name="io", bufs=3) as io,
+        tc.tile_pool(name="work", bufs=3) as work,
+        tc.psum_pool(name="psum", bufs=2) as psum,
+    ):
+        y_of = {}
+        o_of = {}
+        zT_of, zg_of, zq_of, acc1_of, v_of, gap_of, h_of = {}, {}, {}, {}, {}, {}, {}
+        hT_of, hg_of, hq_of, acc2_of = {}, {}, {}, {}
+
+        def load_chunk(c):
+            y_sb = io.tile([P, CHUNK, LANES * FEAT], BF16)
+            nc.sync.dma_start(out=y_sb[:], in_=y_rows[:, CHUNK * c : CHUNK * (c + 1), :])
+            y_of[c] = y_sb
+
+        def store_chunk(c):
+            nc.sync.dma_start(out=out_rows[:, CHUNK * c : CHUNK * (c + 1), :], in_=o_of[c][:])
+
+        load_chunk(0)
+        w1_codes, w1_plane = load_weight(nc, const, w1_words, w1_scales, "w1")
+        w2_codes, w2_plane = load_weight(nc, const, w2_words, w2_scales, "w2")
+        load_chunk(1)
+
+        identity = const.tile([P, P], F32)
+        make_identity(nc, identity[:])
+
+        b1_all = const.tile([P, LANES, FEAT], BF16)
+        nc.scalar.dma_start(
+            out=b1_all[:].rearrange("p g n -> p (g n)"),
+            in_=b1.rearrange("g o n -> (g o n)").partition_broadcast(P),
+        )
+        b2_all = const.tile([P, LANES, FEAT], BF16)
+        nc.scalar.dma_start(
+            out=b2_all[:].rearrange("p g d -> p (g d)"),
+            in_=b2.rearrange("g o d -> (g o d)").partition_broadcast(P),
+        )
+        b2_cols = const.tile([P, FEAT, LANES], BF16)
+        nc.vector.tensor_copy(out=b2_cols[:], in_=b2_all[:].rearrange("p g d -> p d g"))
+
+        def quantise(grouped, label):
+            codes = work.tile([P, LANES * P], U32, name=label + "_codes", align_bytes=64)
+            plane = work.tile([P, LANES * P], U8, name=label + "_plane", align_bytes=64)
+            nc.vector.quantize_mx(
+                out=codes[:].bitcast(FP8X4),
+                scales=plane[:],
+                in_=grouped[:].rearrange("p g b t -> p (g b t)"),
+            )
+            return codes, plane
+
+        def transpose_y(k):
+            y_words = y_of[k // CHUNK][:, k % CHUNK, :].bitcast(F32)
+            zT = psum.tile([P, PACK, P], F32)
+            for t in range(PACK):
+                nc.tensor.transpose(zT[:, t, :], y_words[:, t:FEAT:PACK], identity[:])
+            zT_of[k] = zT
+
+        def split_lanes(k):
+            zg = work.tile([P, LANES, P, PACK], BF16, align_bytes=64)
+            nc.scalar.copy(
+                out=zg[:], in_=zT_of[k][:].bitcast(BF16).rearrange("p t (b g) -> p g b t", g=LANES)
+            )
+            zg_of[k] = zg
+
+        def residual_and_bias(k):
+            c = k // CHUNK
+            if k % CHUNK == 0:
+                o_sb = io.tile([P, CHUNK, LANES * FEAT], F32)
+                o_of[c] = o_sb
+            nc.gpsimd.tensor_tensor(
+                out=o_of[c][:, k % CHUNK, :],
+                in0=y_of[c][:, k % CHUNK, :],
+                in1=b2_cols[:].rearrange("p d g -> p (d g)"),
+                op=ALU.add,
+            )
+
+        def quantise_z(k):
+            zq_of[k] = quantise(zg_of[k], "z")
+
+        def first_matmul(k):
+            z_codes, z_plane = zq_of[k]
+            acc1_of[k] = []
+            for g in range(LANES):
+                rows = slice(g * P, (g + 1) * P)
+                acc1 = psum.tile([P, FEAT], F32)
+                nc.tensor.matmul_mx(
+                    out=acc1[:],
+                    lhsT=z_codes[:, rows].bitcast(FP8X4),
+                    lhsT_scale=z_plane[:, rows],
+                    rhs=w1_codes[:, g, :].bitcast(FP8X4),
+                    rhs_scale=w1_plane[:, g, :],
+                    start=True,
+                    stop=True,
+                )
+                acc1_of[k].append(acc1)
+
+        def add_b1(k):
+            v = work.tile([P, LANES, FEAT], F32)
+            for g in range(LANES):
+                nc.vector.tensor_tensor(
+                    out=v[:, g, :], in0=acc1_of[k][g][:], in1=b1_all[:, g, :], op=ALU.add
+                )
+            v_of[k] = v
+
+        def elu_gap(k):
+            gap = work.tile([P, LANES * FEAT], F32)
+            nc.scalar.activation(out=gap[:], in_=v_of[k][:].rearrange("p g n -> p (g n)"), func=ACT.Exp)
+            nc.scalar.activation(out=gap[:], in_=gap[:], func=ACT.Relu, scale=-1.0, bias=1.0)
+            gap_of[k] = gap
+
+        def elu_max(k):
+            h = work.tile([P, LANES * FEAT], BF16)
+            nc.vector.scalar_tensor_tensor(
+                out=h[:],
+                in0=gap_of[k][:],
+                scalar=-1.0,
+                in1=v_of[k][:].rearrange("p g n -> p (g n)"),
+                op0=ALU.mult,
+                op1=ALU.max,
+            )
+            h_of[k] = h
+
+        def transpose_h(k):
+            h_words = h_of[k][:].bitcast(F32)
+            hT = psum.tile([P, LANES, 2, P], F32)
+            for g in range(LANES):
+                for u in range(2):
+                    nc.tensor.transpose(
+                        hT[:, g, u, :], h_words[:, g * HALF + u : (g + 1) * HALF : 2], identity[:]
+                    )
+            hT_of[k] = hT
+
+        def join_words(k):
+            hg = work.tile([P, LANES, P, PACK], BF16, align_bytes=64)
+            nc.scalar.copy(out=hg[:].bitcast(F32), in_=hT_of[k][:].rearrange("p g u b -> p g b u"))
+            hg_of[k] = hg
+
+        def quantise_h(k):
+            hq_of[k] = quantise(hg_of[k], "h")
+
+        def second_matmul(k):
+            h_codes, h_plane = hq_of[k]
+            acc2_of[k] = []
+            for half in range(2):
+                cols = slice(half * HALF, (half + 1) * HALF)
+                acc2 = psum.tile([P, LANES, HALF], F32)
+                for g in range(LANES):
+                    rows = slice(g * P, (g + 1) * P)
+                    nc.tensor.matmul_mx(
+                        out=acc2[:, g, :],
+                        lhsT=h_codes[:, rows].bitcast(FP8X4),
+                        lhsT_scale=h_plane[:, rows],
+                        rhs=w2_codes[:, g, cols].bitcast(FP8X4),
+                        rhs_scale=w2_plane[:, g, cols],
+                        start=True,
+                        stop=True,
+                    )
+                acc2_of[k].append(acc2)
+
+        def add_to_out(k):
+            o_row = o_of[k // CHUNK][:, k % CHUNK, :]
+            for half in range(2):
+                o_cols = o_row[:, half * FEAT : (half + 1) * FEAT].rearrange("p (d g) -> p d g", g=LANES)
+                nc.vector.tensor_tensor(
+                    out=o_cols, in0=acc2_of[k][half][:].rearrange("p g d -> p d g"), in1=o_cols, op=ALU.add
+                )
+
+        def live(k):
+            return 0 <= k < N_TILES
+
+        for step in range(N_TILES + LAST_STAGE):
+            k0, k1, k2, k3, k4 = step, step - 1, step - 2, step - 3, step - 4
+            if live(k0) and k0 % CHUNK == 0 and k0 // CHUNK + 2 < N_TILES // CHUNK:
+                load_chunk(k0 // CHUNK + 2)
+            if live(k1):
+                quantise_z(k1)
+            if live(k4):
+                quantise_h(k4)
+            if live(k3):
+                elu_max(k3)
+            if live(k1):
+                first_matmul(k1)
+            if live(k4):
+                second_matmul(k4)
+            if live(k0):
+                transpose_y(k0)
+            if live(k3):
+                transpose_h(k3)
+            if live(k2):
+                elu_gap(k2)
+            if live(k1):
+                add_b1(k1)
+            if live(k4):
+                add_to_out(k4)
+                if k4 % CHUNK == CHUNK - 1:
+                    store_chunk(k4 // CHUNK)
+            if live(k0):
+                split_lanes(k0)
+                residual_and_bias(k0)
+            if live(k3):
+                join_words(k3)

@@ -15,10 +15,11 @@ PACK = 4
 LANES = 2
 ROWS = 4096
 FEAT = 512
-HALF = FEAT // 2
 N_TILES = ROWS // P
 CHUNK = 4
-LAST_STAGE = 4
+BLOCKS = FEAT // P
+AHEAD = 4
+assert BLOCKS == CHUNK
 
 FLOPS = 2 * 2 * LANES * ROWS * FEAT * FEAT
 
@@ -48,27 +49,26 @@ def tile_blockresmlp_mixerblock_pa_t_e_kernel(
 
     with (
         tc.tile_pool(name="const", bufs=1) as const,
-        tc.tile_pool(name="io", bufs=3) as io,
+        tc.tile_pool(name="rows", bufs=5) as rows_pool,
         tc.tile_pool(name="work", bufs=3) as work,
+        tc.tile_pool(name="chunked", bufs=2) as chunked,
         tc.psum_pool(name="psum", bufs=2) as psum,
     ):
-        y_of = {}
-        o_of = {}
-        zT_of, zg_of, zq_of, acc1_of, v_of, gap_of, h_of = {}, {}, {}, {}, {}, {}, {}
-        hT_of, hg_of, hq_of, acc2_of = {}, {}, {}, {}
+        y_of, hq_of, o_of = {}, {}, {}
+        zT_of, zg_of, zq_of, acc1_of, v_of, low_of, h_of, hT_of, hg_of = {}, {}, {}, {}, {}, {}, {}, {}, {}
+        acc2_of, r_of, back_of = {}, {}, {}
 
-        def load_chunk(c):
-            y_sb = io.tile([P, CHUNK, LANES * FEAT], BF16)
-            nc.sync.dma_start(out=y_sb[:], in_=y_rows[:, CHUNK * c : CHUNK * (c + 1), :])
-            y_of[c] = y_sb
+        def load_rows(k):
+            if k % CHUNK == 0:
+                y_sb = rows_pool.tile([P, CHUNK, LANES * FEAT], BF16)
+                y_of[k // CHUNK] = y_sb
+            nc.sync.dma_start(out=y_of[k // CHUNK][:, k % CHUNK, :], in_=y_rows[:, k, :])
 
-        def store_chunk(c):
-            nc.sync.dma_start(out=out_rows[:, CHUNK * c : CHUNK * (c + 1), :], in_=o_of[c][:])
-
-        load_chunk(0)
+        load_rows(0)
         w1_codes, w1_plane = load_weight(nc, const, w1_words, w1_scales, "w1")
+        for k in range(1, AHEAD):
+            load_rows(k)
         w2_codes, w2_plane = load_weight(nc, const, w2_words, w2_scales, "w2")
-        load_chunk(1)
 
         identity = const.tile([P, P], F32)
         make_identity(nc, identity[:])
@@ -78,27 +78,21 @@ def tile_blockresmlp_mixerblock_pa_t_e_kernel(
             out=b1_all[:].rearrange("p g n -> p (g n)"),
             in_=b1.rearrange("g o n -> (g o n)").partition_broadcast(P),
         )
-        b2_all = const.tile([P, LANES, FEAT], BF16)
+        b2_rows = const.tile([P, P], BF16)
+        nc.vector.memset(b2_rows[:], 0.0)
         nc.scalar.dma_start(
-            out=b2_all[:].rearrange("p g d -> p (g d)"),
-            in_=b2.rearrange("g o d -> (g o d)").partition_broadcast(P),
+            out=b2_rows[0 : LANES * BLOCKS, :], in_=b2.rearrange("g o (j m) -> (g o j) m", m=P)
         )
-        b2_cols = const.tile([P, FEAT, LANES], BF16)
-        nc.vector.tensor_copy(out=b2_cols[:], in_=b2_all[:].rearrange("p g d -> p d g"))
-
-        def quantise(grouped, label):
-            codes = work.tile([P, LANES * P], U32, name=label + "_codes", align_bytes=64)
-            plane = work.tile([P, LANES * P], U8, name=label + "_plane", align_bytes=64)
-            nc.vector.quantize_mx(
-                out=codes[:].bitcast(FP8X4),
-                scales=plane[:],
-                in_=grouped[:].rearrange("p g b t -> p (g b t)"),
-            )
-            return codes, plane
+        b2_wide = const.tile([P, P], F32)
+        nc.vector.tensor_copy(out=b2_wide[:], in_=b2_rows[:])
+        b2_turned = psum.tile([P, P], F32, tag="hT", bufs=1)
+        nc.tensor.transpose(b2_turned[:], b2_wide[:], identity[:])
+        b2_col = const.tile([P, LANES * BLOCKS], F32)
+        nc.vector.tensor_copy(out=b2_col[:], in_=b2_turned[:, 0 : LANES * BLOCKS])
 
         def transpose_y(k):
             y_words = y_of[k // CHUNK][:, k % CHUNK, :].bitcast(F32)
-            zT = psum.tile([P, PACK, P], F32)
+            zT = psum.tile([P, PACK, P], F32, bufs=1)
             for t in range(PACK):
                 nc.tensor.transpose(zT[:, t, :], y_words[:, t:FEAT:PACK], identity[:])
             zT_of[k] = zT
@@ -110,20 +104,15 @@ def tile_blockresmlp_mixerblock_pa_t_e_kernel(
             )
             zg_of[k] = zg
 
-        def residual_and_bias(k):
-            c = k // CHUNK
-            if k % CHUNK == 0:
-                o_sb = io.tile([P, CHUNK, LANES * FEAT], F32)
-                o_of[c] = o_sb
-            nc.gpsimd.tensor_tensor(
-                out=o_of[c][:, k % CHUNK, :],
-                in0=y_of[c][:, k % CHUNK, :],
-                in1=b2_cols[:].rearrange("p d g -> p (d g)"),
-                op=ALU.add,
-            )
-
         def quantise_z(k):
-            zq_of[k] = quantise(zg_of[k], "z")
+            z_codes = work.tile([P, LANES * P], U32, align_bytes=64)
+            z_plane = work.tile([P, LANES * P], U8, align_bytes=64)
+            nc.vector.quantize_mx(
+                out=z_codes[:].bitcast(FP8X4),
+                scales=z_plane[:],
+                in_=zg_of[k][:].rearrange("p g b t -> p (g b t)"),
+            )
+            zq_of[k] = (z_codes, z_plane)
 
         def first_matmul(k):
             z_codes, z_plane = zq_of[k]
@@ -150,31 +139,34 @@ def tile_blockresmlp_mixerblock_pa_t_e_kernel(
                 )
             v_of[k] = v
 
-        def elu_gap(k):
-            gap = work.tile([P, LANES * FEAT], F32)
-            nc.scalar.activation(out=gap[:], in_=v_of[k][:].rearrange("p g n -> p (g n)"), func=ACT.Exp)
-            nc.scalar.activation(out=gap[:], in_=gap[:], func=ACT.Relu, scale=-1.0, bias=1.0)
-            gap_of[k] = gap
+        def elu_low(k):
+            low = work.tile([P, LANES * FEAT], F32)
+            nc.scalar.activation(out=low[:], in_=v_of[k][:].rearrange("p g n -> p (g n)"), func=ACT.Exp)
+            nc.gpsimd.tensor_scalar(
+                out=low[:], in0=low[:], scalar1=1.0, scalar2=0.0, op0=ALU.min, op1=ALU.max
+            )
+            low_of[k] = low
 
         def elu_max(k):
             h = work.tile([P, LANES * FEAT], BF16)
             nc.vector.scalar_tensor_tensor(
                 out=h[:],
-                in0=gap_of[k][:],
+                in0=low_of[k][:],
                 scalar=-1.0,
                 in1=v_of[k][:].rearrange("p g n -> p (g n)"),
-                op0=ALU.mult,
+                op0=ALU.add,
                 op1=ALU.max,
             )
             h_of[k] = h
 
         def transpose_h(k):
             h_words = h_of[k][:].bitcast(F32)
-            hT = psum.tile([P, LANES, 2, P], F32)
+            words = FEAT // 2
+            hT = psum.tile([P, LANES, 2, P], F32, bufs=1)
             for g in range(LANES):
                 for u in range(2):
                     nc.tensor.transpose(
-                        hT[:, g, u, :], h_words[:, g * HALF + u : (g + 1) * HALF : 2], identity[:]
+                        hT[:, g, u, :], h_words[:, g * words + u : (g + 1) * words : 2], identity[:]
                     )
             hT_of[k] = hT
 
@@ -184,66 +176,109 @@ def tile_blockresmlp_mixerblock_pa_t_e_kernel(
             hg_of[k] = hg
 
         def quantise_h(k):
-            hq_of[k] = quantise(hg_of[k], "h")
-
-        def second_matmul(k):
-            h_codes, h_plane = hq_of[k]
-            acc2_of[k] = []
-            for half in range(2):
-                cols = slice(half * HALF, (half + 1) * HALF)
-                acc2 = psum.tile([P, LANES, HALF], F32)
-                for g in range(LANES):
-                    rows = slice(g * P, (g + 1) * P)
-                    nc.tensor.matmul_mx(
-                        out=acc2[:, g, :],
-                        lhsT=h_codes[:, rows].bitcast(FP8X4),
-                        lhsT_scale=h_plane[:, rows],
-                        rhs=w2_codes[:, g, cols].bitcast(FP8X4),
-                        rhs_scale=w2_plane[:, g, cols],
-                        start=True,
-                        stop=True,
-                    )
-                acc2_of[k].append(acc2)
-
-        def add_to_out(k):
-            o_row = o_of[k // CHUNK][:, k % CHUNK, :]
-            for half in range(2):
-                o_cols = o_row[:, half * FEAT : (half + 1) * FEAT].rearrange("p (d g) -> p d g", g=LANES)
-                nc.vector.tensor_tensor(
-                    out=o_cols, in0=acc2_of[k][half][:].rearrange("p g d -> p d g"), in1=o_cols, op=ALU.add
+            if k % CHUNK == 0:
+                h_codes = chunked.tile([P, LANES, CHUNK * P], U32, align_bytes=64)
+                h_plane = chunked.tile([P, LANES, CHUNK * P], U8, align_bytes=64)
+                hq_of[k // CHUNK] = (h_codes, h_plane)
+            h_codes, h_plane = hq_of[k // CHUNK]
+            rows = slice((k % CHUNK) * P, (k % CHUNK + 1) * P)
+            for g in range(LANES):
+                nc.vector.quantize_mx(
+                    out=h_codes[:, g, rows].bitcast(FP8X4),
+                    scales=h_plane[:, g, rows],
+                    in_=hg_of[k][:, g, :, :].rearrange("p b t -> p (b t)"),
                 )
+
+        def second_matmul(c, j):
+            h_codes, h_plane = hq_of[c]
+            feats = slice(j * P, (j + 1) * P)
+            acc2_of[c, j] = []
+            for g in range(LANES):
+                acc2 = psum.tile([P, CHUNK * P], F32)
+                nc.tensor.matmul_mx(
+                    out=acc2[:],
+                    lhsT=w2_codes[:, g, feats].bitcast(FP8X4),
+                    lhsT_scale=w2_plane[:, g, feats],
+                    rhs=h_codes[:, g, :].bitcast(FP8X4),
+                    rhs_scale=h_plane[:, g, :],
+                    start=True,
+                    stop=True,
+                )
+                acc2_of[c, j].append(acc2)
+
+        def add_b2(c, j):
+            r = chunked.tile([P, LANES, CHUNK * P], F32)
+            for g in range(LANES):
+                nc.scalar.activation(
+                    out=r[:, g, :],
+                    in_=acc2_of[c, j][g][:],
+                    func=ACT.Identity,
+                    bias=b2_col[:, BLOCKS * g + j : BLOCKS * g + j + 1],
+                )
+            r_of[c, j] = r
+
+        def transpose_back(c, j):
+            back_of[c, j] = []
+            for pair in range(CHUNK // 2):
+                back = psum.tile([P, 2, LANES, P], F32)
+                for i in range(2):
+                    rows = slice((2 * pair + i) * P, (2 * pair + i + 1) * P)
+                    for g in range(LANES):
+                        nc.tensor.transpose(back[:, i, g, :], r_of[c, j][:, g, rows], identity[:])
+                back_of[c, j].append(back)
+
+        def add_y_and_store(c, j):
+            if j == 0:
+                o_sb = chunked.tile([P, CHUNK, LANES * FEAT], F32)
+                o_of[c] = o_sb
+            cols = slice(j * LANES * P, (j + 1) * LANES * P)
+            for pair in range(CHUNK // 2):
+                tiles = slice(2 * pair, 2 * pair + 2)
+                nc.vector.tensor_tensor(
+                    out=o_of[c][:, tiles, cols].rearrange("p i (m g) -> p i m g", g=LANES),
+                    in0=back_of[c, j][pair][:].rearrange("p i g m -> p i m g"),
+                    in1=y_of[c][:, tiles, cols].rearrange("p i (m g) -> p i m g", g=LANES),
+                    op=ALU.add,
+                )
+            nc.sync.dma_start(
+                out=out_rows[:, CHUNK * c : CHUNK * (c + 1), cols], in_=o_of[c][:, :, cols]
+            )
 
         def live(k):
             return 0 <= k < N_TILES
 
-        for step in range(N_TILES + LAST_STAGE):
-            k0, k1, k2, k3, k4 = step, step - 1, step - 2, step - 3, step - 4
-            if live(k0) and k0 % CHUNK == 0 and k0 // CHUNK + 2 < N_TILES // CHUNK:
-                load_chunk(k0 // CHUNK + 2)
-            if live(k1):
-                quantise_z(k1)
-            if live(k4):
-                quantise_h(k4)
-            if live(k3):
-                elu_max(k3)
-            if live(k1):
-                first_matmul(k1)
-            if live(k4):
-                second_matmul(k4)
-            if live(k0):
-                transpose_y(k0)
-            if live(k3):
-                transpose_h(k3)
-            if live(k2):
-                elu_gap(k2)
-            if live(k1):
-                add_b1(k1)
-            if live(k4):
-                add_to_out(k4)
-                if k4 % CHUNK == CHUNK - 1:
-                    store_chunk(k4 // CHUNK)
-            if live(k0):
-                split_lanes(k0)
-                residual_and_bias(k0)
-            if live(k3):
-                join_words(k3)
+        first_block_round = CHUNK - 1 + 4
+        with tc.manual_schedule():
+            for step in range(N_TILES + first_block_round + 1):
+                k0, k1, k2, k3, k4 = step, step - 1, step - 2, step - 3, step - 4
+                u5, u6 = step - first_block_round, step - first_block_round - 1
+                if live(k0 + AHEAD):
+                    load_rows(k0 + AHEAD)
+                if live(k1):
+                    quantise_z(k1)
+                if live(k4):
+                    quantise_h(k4)
+                if live(k3):
+                    elu_max(k3)
+                if live(u6):
+                    transpose_back(u6 // BLOCKS, u6 % BLOCKS)
+                if live(k1):
+                    first_matmul(k1)
+                if live(u5):
+                    second_matmul(u5 // BLOCKS, u5 % BLOCKS)
+                if live(k0):
+                    transpose_y(k0)
+                if live(k3):
+                    transpose_h(k3)
+                if live(k2):
+                    elu_low(k2)
+                if live(u5):
+                    add_b2(u5 // BLOCKS, u5 % BLOCKS)
+                if live(u6):
+                    add_y_and_store(u6 // BLOCKS, u6 % BLOCKS)
+                if live(k1):
+                    add_b1(k1)
+                if live(k0):
+                    split_lanes(k0)
+                if live(k3):
+                    join_words(k3)

@@ -16,10 +16,10 @@ LANES = 2
 ROWS = 4096
 FEAT = 512
 N_TILES = ROWS // P
-CHUNK = 4
-BLOCKS = FEAT // P
+HALF = FEAT // 2
 AHEAD = 4
-assert BLOCKS == CHUNK
+LAST_STAGE = 6
+PIECES = 4
 
 FLOPS = 2 * 2 * LANES * ROWS * FEAT * FEAT
 
@@ -44,25 +44,21 @@ def tile_blockresmlp_mixerblock_pa_t_e_kernel(
     tc, y_lanes, w1_words, w1_scales, b1, w2_words, w2_scales, b2, out
 ):
     nc = tc.nc
-    y_rows = y_lanes.rearrange("(p k) c -> p k c", k=N_TILES)
-    out_rows = out.rearrange("(p k) c -> p k c", k=N_TILES)
 
     with (
         tc.tile_pool(name="const", bufs=1) as const,
-        tc.tile_pool(name="rows", bufs=5) as rows_pool,
+        tc.tile_pool(name="rows_in", bufs=AHEAD + LAST_STAGE) as rows_in,
+        tc.tile_pool(name="rows_out", bufs=4) as rows_out,
         tc.tile_pool(name="work", bufs=3) as work,
-        tc.tile_pool(name="chunked", bufs=2) as chunked,
         tc.psum_pool(name="psum", bufs=2) as psum,
     ):
-        y_of, hq_of, o_of = {}, {}, {}
-        zT_of, zg_of, zq_of, acc1_of, v_of, low_of, h_of, hT_of, hg_of = {}, {}, {}, {}, {}, {}, {}, {}, {}
-        acc2_of, r_of, back_of = {}, {}, {}
+        y_of, zT_of, zg_of, zq_of, acc1_of, v_of, gap_of, h_of = {}, {}, {}, {}, {}, {}, {}, {}
+        hT_of, hg_of, hq_of, acc2_of, o_of = {}, {}, {}, {}, {}
 
         def load_rows(k):
-            if k % CHUNK == 0:
-                y_sb = rows_pool.tile([P, CHUNK, LANES * FEAT], BF16)
-                y_of[k // CHUNK] = y_sb
-            nc.sync.dma_start(out=y_of[k // CHUNK][:, k % CHUNK, :], in_=y_rows[:, k, :])
+            y_sb = rows_in.tile([P, LANES * FEAT], BF16)
+            nc.sync.dma_start(out=y_sb[:], in_=y_lanes[k * P : (k + 1) * P, :])
+            y_of[k] = y_sb
 
         load_rows(0)
         w1_codes, w1_plane = load_weight(nc, const, w1_words, w1_scales, "w1")
@@ -78,21 +74,27 @@ def tile_blockresmlp_mixerblock_pa_t_e_kernel(
             out=b1_all[:].rearrange("p g n -> p (g n)"),
             in_=b1.rearrange("g o n -> (g o n)").partition_broadcast(P),
         )
-        b2_rows = const.tile([P, P], BF16)
-        nc.vector.memset(b2_rows[:], 0.0)
+        b2_all = const.tile([P, LANES, FEAT], BF16)
         nc.scalar.dma_start(
-            out=b2_rows[0 : LANES * BLOCKS, :], in_=b2.rearrange("g o (j m) -> (g o j) m", m=P)
+            out=b2_all[:].rearrange("p g d -> p (g d)"),
+            in_=b2.rearrange("g o d -> (g o d)").partition_broadcast(P),
         )
-        b2_wide = const.tile([P, P], F32)
-        nc.vector.tensor_copy(out=b2_wide[:], in_=b2_rows[:])
-        b2_turned = psum.tile([P, P], F32, tag="hT", bufs=1)
-        nc.tensor.transpose(b2_turned[:], b2_wide[:], identity[:])
-        b2_col = const.tile([P, LANES * BLOCKS], F32)
-        nc.vector.tensor_copy(out=b2_col[:], in_=b2_turned[:, 0 : LANES * BLOCKS])
+        b2_cols = const.tile([P, FEAT, LANES], BF16)
+        nc.vector.tensor_copy(out=b2_cols[:], in_=b2_all[:].rearrange("p g d -> p d g"))
+
+        def quantise(grouped, label):
+            codes = work.tile([P, LANES * P], U32, name=label + "_codes", align_bytes=64)
+            plane = work.tile([P, LANES * P], U8, name=label + "_plane", align_bytes=64)
+            nc.vector.quantize_mx(
+                out=codes[:].bitcast(FP8X4),
+                scales=plane[:],
+                in_=grouped[:].rearrange("p g b t -> p (g b t)"),
+            )
+            return codes, plane
 
         def transpose_y(k):
-            y_words = y_of[k // CHUNK][:, k % CHUNK, :].bitcast(F32)
-            zT = psum.tile([P, PACK, P], F32, bufs=1)
+            y_words = y_of[k][:].bitcast(F32)
+            zT = psum.tile([P, PACK, P], F32)
             for t in range(PACK):
                 nc.tensor.transpose(zT[:, t, :], y_words[:, t:FEAT:PACK], identity[:])
             zT_of[k] = zT
@@ -105,14 +107,7 @@ def tile_blockresmlp_mixerblock_pa_t_e_kernel(
             zg_of[k] = zg
 
         def quantise_z(k):
-            z_codes = work.tile([P, LANES * P], U32, align_bytes=64)
-            z_plane = work.tile([P, LANES * P], U8, align_bytes=64)
-            nc.vector.quantize_mx(
-                out=z_codes[:].bitcast(FP8X4),
-                scales=z_plane[:],
-                in_=zg_of[k][:].rearrange("p g b t -> p (g b t)"),
-            )
-            zq_of[k] = (z_codes, z_plane)
+            zq_of[k] = quantise(zg_of[k], "z")
 
         def first_matmul(k):
             z_codes, z_plane = zq_of[k]
@@ -139,34 +134,31 @@ def tile_blockresmlp_mixerblock_pa_t_e_kernel(
                 )
             v_of[k] = v
 
-        def elu_low(k):
-            low = work.tile([P, LANES * FEAT], F32)
-            nc.scalar.activation(out=low[:], in_=v_of[k][:].rearrange("p g n -> p (g n)"), func=ACT.Exp)
-            nc.gpsimd.tensor_scalar(
-                out=low[:], in0=low[:], scalar1=1.0, scalar2=0.0, op0=ALU.min, op1=ALU.max
-            )
-            low_of[k] = low
+        def elu_gap(k):
+            gap = work.tile([P, LANES * FEAT], F32)
+            nc.scalar.activation(out=gap[:], in_=v_of[k][:].rearrange("p g n -> p (g n)"), func=ACT.Exp)
+            nc.scalar.activation(out=gap[:], in_=gap[:], func=ACT.Relu, scale=-1.0, bias=1.0)
+            gap_of[k] = gap
 
         def elu_max(k):
             h = work.tile([P, LANES * FEAT], BF16)
             nc.vector.scalar_tensor_tensor(
                 out=h[:],
-                in0=low_of[k][:],
+                in0=gap_of[k][:],
                 scalar=-1.0,
                 in1=v_of[k][:].rearrange("p g n -> p (g n)"),
-                op0=ALU.add,
+                op0=ALU.mult,
                 op1=ALU.max,
             )
             h_of[k] = h
 
         def transpose_h(k):
             h_words = h_of[k][:].bitcast(F32)
-            words = FEAT // 2
-            hT = psum.tile([P, LANES, 2, P], F32, bufs=1)
+            hT = psum.tile([P, LANES, 2, P], F32)
             for g in range(LANES):
                 for u in range(2):
                     nc.tensor.transpose(
-                        hT[:, g, u, :], h_words[:, g * words + u : (g + 1) * words : 2], identity[:]
+                        hT[:, g, u, :], h_words[:, g * HALF + u : (g + 1) * HALF : 2], identity[:]
                     )
             hT_of[k] = hT
 
@@ -175,110 +167,80 @@ def tile_blockresmlp_mixerblock_pa_t_e_kernel(
             nc.scalar.copy(out=hg[:].bitcast(F32), in_=hT_of[k][:].rearrange("p g u b -> p g b u"))
             hg_of[k] = hg
 
-        def quantise_h(k):
-            if k % CHUNK == 0:
-                h_codes = chunked.tile([P, LANES, CHUNK * P], U32, align_bytes=64)
-                h_plane = chunked.tile([P, LANES, CHUNK * P], U8, align_bytes=64)
-                hq_of[k // CHUNK] = (h_codes, h_plane)
-            h_codes, h_plane = hq_of[k // CHUNK]
-            rows = slice((k % CHUNK) * P, (k % CHUNK + 1) * P)
-            for g in range(LANES):
-                nc.vector.quantize_mx(
-                    out=h_codes[:, g, rows].bitcast(FP8X4),
-                    scales=h_plane[:, g, rows],
-                    in_=hg_of[k][:, g, :, :].rearrange("p b t -> p (b t)"),
-                )
-
-        def second_matmul(c, j):
-            h_codes, h_plane = hq_of[c]
-            feats = slice(j * P, (j + 1) * P)
-            acc2_of[c, j] = []
-            for g in range(LANES):
-                acc2 = psum.tile([P, CHUNK * P], F32)
-                nc.tensor.matmul_mx(
-                    out=acc2[:],
-                    lhsT=w2_codes[:, g, feats].bitcast(FP8X4),
-                    lhsT_scale=w2_plane[:, g, feats],
-                    rhs=h_codes[:, g, :].bitcast(FP8X4),
-                    rhs_scale=h_plane[:, g, :],
-                    start=True,
-                    stop=True,
-                )
-                acc2_of[c, j].append(acc2)
-
-        def add_b2(c, j):
-            r = chunked.tile([P, LANES, CHUNK * P], F32)
-            for g in range(LANES):
-                nc.scalar.activation(
-                    out=r[:, g, :],
-                    in_=acc2_of[c, j][g][:],
-                    func=ACT.Identity,
-                    bias=b2_col[:, BLOCKS * g + j : BLOCKS * g + j + 1],
-                )
-            r_of[c, j] = r
-
-        def transpose_back(c, j):
-            back_of[c, j] = []
-            for pair in range(CHUNK // 2):
-                back = psum.tile([P, 2, LANES, P], F32)
-                for i in range(2):
-                    rows = slice((2 * pair + i) * P, (2 * pair + i + 1) * P)
-                    for g in range(LANES):
-                        nc.tensor.transpose(back[:, i, g, :], r_of[c, j][:, g, rows], identity[:])
-                back_of[c, j].append(back)
-
-        def add_y_and_store(c, j):
-            if j == 0:
-                o_sb = chunked.tile([P, CHUNK, LANES * FEAT], F32)
-                o_of[c] = o_sb
-            cols = slice(j * LANES * P, (j + 1) * LANES * P)
-            for pair in range(CHUNK // 2):
-                tiles = slice(2 * pair, 2 * pair + 2)
-                nc.vector.tensor_tensor(
-                    out=o_of[c][:, tiles, cols].rearrange("p i (m g) -> p i m g", g=LANES),
-                    in0=back_of[c, j][pair][:].rearrange("p i g m -> p i m g"),
-                    in1=y_of[c][:, tiles, cols].rearrange("p i (m g) -> p i m g", g=LANES),
+        def residual_and_bias(k):
+            o_sb = rows_out.tile([P, LANES * FEAT], F32)
+            width = LANES * FEAT // PIECES
+            for piece in range(PIECES):
+                cols = slice(piece * width, (piece + 1) * width)
+                nc.gpsimd.tensor_tensor(
+                    out=o_sb[:, cols],
+                    in0=y_of[k][:, cols],
+                    in1=b2_cols[:].rearrange("p d g -> p (d g)")[:, cols],
                     op=ALU.add,
                 )
-            nc.sync.dma_start(
-                out=out_rows[:, CHUNK * c : CHUNK * (c + 1), cols], in_=o_of[c][:, :, cols]
-            )
+            o_of[k] = o_sb
+
+        def quantise_h(k):
+            hq_of[k] = quantise(hg_of[k], "h")
+
+        def second_matmul(k):
+            h_codes, h_plane = hq_of[k]
+            acc2_of[k] = []
+            for half in range(2):
+                cols = slice(half * HALF, (half + 1) * HALF)
+                acc2 = psum.tile([P, LANES, HALF], F32)
+                for g in range(LANES):
+                    rows = slice(g * P, (g + 1) * P)
+                    nc.tensor.matmul_mx(
+                        out=acc2[:, g, :],
+                        lhsT=h_codes[:, rows].bitcast(FP8X4),
+                        lhsT_scale=h_plane[:, rows],
+                        rhs=w2_codes[:, g, cols].bitcast(FP8X4),
+                        rhs_scale=w2_plane[:, g, cols],
+                        start=True,
+                        stop=True,
+                    )
+                acc2_of[k].append(acc2)
+
+        def add_to_out_and_store(k):
+            for half in range(2):
+                o_cols = o_of[k][:, half * FEAT : (half + 1) * FEAT].rearrange("p (d g) -> p d g", g=LANES)
+                nc.vector.tensor_tensor(
+                    out=o_cols, in0=acc2_of[k][half][:].rearrange("p g d -> p d g"), in1=o_cols, op=ALU.add
+                )
+            nc.sync.dma_start(out=out[k * P : (k + 1) * P, :], in_=o_of[k][:])
 
         def live(k):
             return 0 <= k < N_TILES
 
-        first_block_round = CHUNK - 1 + 4
         with tc.manual_schedule():
-            for step in range(N_TILES + first_block_round + 1):
-                k0, k1, k2, k3, k4 = step, step - 1, step - 2, step - 3, step - 4
-                u5, u6 = step - first_block_round, step - first_block_round - 1
+            for step in range(N_TILES + LAST_STAGE):
+                k0, k1, k2, k3 = step, step - 1, step - 2, step - 3
+                k4, k5, k6 = step - 4, step - 5, step - 6
                 if live(k0 + AHEAD):
                     load_rows(k0 + AHEAD)
-                if live(k1):
-                    quantise_z(k1)
+                if live(k2):
+                    quantise_z(k2)
+                if live(k6):
+                    quantise_h(k6)
                 if live(k4):
-                    quantise_h(k4)
-                if live(k3):
-                    elu_max(k3)
-                if live(u6):
-                    transpose_back(u6 // BLOCKS, u6 % BLOCKS)
-                if live(k1):
-                    first_matmul(k1)
-                if live(u5):
-                    second_matmul(u5 // BLOCKS, u5 % BLOCKS)
+                    elu_max(k4)
+                if live(k2):
+                    first_matmul(k2)
                 if live(k0):
                     transpose_y(k0)
-                if live(k3):
-                    transpose_h(k3)
-                if live(k2):
-                    elu_low(k2)
-                if live(u5):
-                    add_b2(u5 // BLOCKS, u5 % BLOCKS)
-                if live(u6):
-                    add_y_and_store(u6 // BLOCKS, u6 % BLOCKS)
+                if live(k4):
+                    transpose_h(k4)
+                if live(k6):
+                    second_matmul(k6)
                 if live(k1):
-                    add_b1(k1)
-                if live(k0):
-                    split_lanes(k0)
+                    split_lanes(k1)
+                if live(k5):
+                    join_words(k5)
+                    residual_and_bias(k5)
                 if live(k3):
-                    join_words(k3)
+                    elu_gap(k3)
+                if live(k2):
+                    add_b1(k2)
+                if live(k6):
+                    add_to_out_and_store(k6)

@@ -164,7 +164,7 @@ def tile_blockresmlp_mixerblock_pa_t_e_kernel(
 
         def join_words(k):
             hg = work.tile([P, LANES, P, PACK], BF16, align_bytes=64)
-            nc.scalar.copy(out=hg[:].bitcast(F32), in_=hT_of[k][:].rearrange("p g u b -> p g b u"))
+            nc.vector.tensor_copy(out=hg[:].bitcast(F32), in_=hT_of[k][:].rearrange("p g u b -> p g b u"))
             hg_of[k] = hg
 
         def residual_and_bias(k):
@@ -236,10 +236,11 @@ def tile_blockresmlp_mixerblock_pa_t_e_kernel(
                 if live(k1):
                     split_lanes(k1)
                 if live(k5):
-                    join_words(k5)
                     residual_and_bias(k5)
                 if live(k3):
                     elu_gap(k3)
+                if live(k5):
+                    join_words(k5)
                 if live(k2):
                     add_b1(k2)
                 if live(k6):

@@ -18,8 +18,8 @@ FEAT = 512
 N_TILES = ROWS // P
 HALF = FEAT // 2
 AHEAD = 4
-LAST_STAGE = 6
-PIECES = 4
+LAST_STAGE = 7
+PIECES = 2
 
 FLOPS = 2 * 2 * LANES * ROWS * FEAT * FEAT
 
@@ -47,8 +47,8 @@ def tile_blockresmlp_mixerblock_pa_t_e_kernel(
 
     with (
         tc.tile_pool(name="const", bufs=1) as const,
-        tc.tile_pool(name="rows_in", bufs=AHEAD + LAST_STAGE) as rows_in,
-        tc.tile_pool(name="rows_out", bufs=4) as rows_out,
+        tc.tile_pool(name="rows_in", bufs=AHEAD + 5) as rows_in,
+        tc.tile_pool(name="rows_f32", bufs=8) as rows_f32,
         tc.tile_pool(name="work", bufs=3) as work,
         tc.psum_pool(name="psum", bufs=2) as psum,
     ):
@@ -94,7 +94,7 @@ def tile_blockresmlp_mixerblock_pa_t_e_kernel(
 
         def transpose_y(k):
             y_words = y_of[k][:].bitcast(F32)
-            zT = psum.tile([P, PACK, P], F32)
+            zT = psum.tile([P, PACK, P], F32, bufs=1)
             for t in range(PACK):
                 nc.tensor.transpose(zT[:, t, :], y_words[:, t:FEAT:PACK], identity[:])
             zT_of[k] = zT
@@ -127,7 +127,7 @@ def tile_blockresmlp_mixerblock_pa_t_e_kernel(
                 acc1_of[k].append(acc1)
 
         def add_b1(k):
-            v = work.tile([P, LANES, FEAT], F32)
+            v = rows_f32.tile([P, LANES, FEAT], F32)
             for g in range(LANES):
                 nc.vector.tensor_tensor(
                     out=v[:, g, :], in0=acc1_of[k][g][:], in1=b1_all[:, g, :], op=ALU.add
@@ -154,7 +154,7 @@ def tile_blockresmlp_mixerblock_pa_t_e_kernel(
 
         def transpose_h(k):
             h_words = h_of[k][:].bitcast(F32)
-            hT = psum.tile([P, LANES, 2, P], F32)
+            hT = psum.tile([P, LANES, 2, P], F32, bufs=1)
             for g in range(LANES):
                 for u in range(2):
                     nc.tensor.transpose(
@@ -164,11 +164,11 @@ def tile_blockresmlp_mixerblock_pa_t_e_kernel(
 
         def join_words(k):
             hg = work.tile([P, LANES, P, PACK], BF16, align_bytes=64)
-            nc.vector.tensor_copy(out=hg[:].bitcast(F32), in_=hT_of[k][:].rearrange("p g u b -> p g b u"))
+            nc.scalar.copy(out=hg[:].bitcast(F32), in_=hT_of[k][:].rearrange("p g u b -> p g b u"))
             hg_of[k] = hg
 
         def residual_and_bias(k):
-            o_sb = rows_out.tile([P, LANES * FEAT], F32)
+            o_sb = v_of[k][:].rearrange("p g n -> p (g n)")
             width = LANES * FEAT // PIECES
             for piece in range(PIECES):
                 cols = slice(piece * width, (piece + 1) * width)
@@ -188,7 +188,7 @@ def tile_blockresmlp_mixerblock_pa_t_e_kernel(
             acc2_of[k] = []
             for half in range(2):
                 cols = slice(half * HALF, (half + 1) * HALF)
-                acc2 = psum.tile([P, LANES, HALF], F32)
+                acc2 = psum.tile([P, LANES, HALF], F32, bufs=4)
                 for g in range(LANES):
                     rows = slice(g * P, (g + 1) * P)
                     nc.tensor.matmul_mx(
@@ -216,32 +216,31 @@ def tile_blockresmlp_mixerblock_pa_t_e_kernel(
         with tc.manual_schedule():
             for step in range(N_TILES + LAST_STAGE):
                 k0, k1, k2, k3 = step, step - 1, step - 2, step - 3
-                k4, k5, k6 = step - 4, step - 5, step - 6
+                k4, k5, k6, k7 = step - 4, step - 5, step - 6, step - 7
                 if live(k0 + AHEAD):
                     load_rows(k0 + AHEAD)
+                if live(k1):
+                    split_lanes(k1)
+                if live(k5):
+                    join_words(k5)
                 if live(k2):
                     quantise_z(k2)
                 if live(k6):
                     quantise_h(k6)
                 if live(k4):
                     elu_max(k4)
+                    residual_and_bias(k4)
                 if live(k2):
                     first_matmul(k2)
+                if live(k6):
+                    second_matmul(k6)
                 if live(k0):
                     transpose_y(k0)
                 if live(k4):
                     transpose_h(k4)
-                if live(k6):
-                    second_matmul(k6)
-                if live(k1):
-                    split_lanes(k1)
-                if live(k5):
-                    residual_and_bias(k5)
                 if live(k3):
                     elu_gap(k3)
-                if live(k5):
-                    join_words(k5)
+                if live(k7):
+                    add_to_out_and_store(k7)
                 if live(k2):
                     add_b1(k2)
-                if live(k6):
-                    add_to_out_and_store(k6)

@@ -12,14 +12,18 @@ ALU = mybir.AluOpType
 
 P = 128
 PACK = 4
+PAIRS = PACK // 2
 LANES = 2
 ROWS = 4096
 FEAT = 512
 N_TILES = ROWS // P
-HALF = FEAT // 2
+HALVES = 2
+HALF = FEAT // HALVES
+QUADRANTS = 4
+QUADRANT = P // QUADRANTS
+SCALE_ROWS = 4
 AHEAD = 4
 LAST_STAGE = 7
-PIECES = 2
 
 FLOPS = 2 * 2 * LANES * ROWS * FEAT * FEAT
 
@@ -32,10 +36,12 @@ def load_weight(nc, pool, words, scales, label):
         out=codes[:].bitcast(I32),
         in_=words.rearrange("g p n t -> p g (n t)").bitcast(I32),
     )
-    for quadrant in range(4):
+    for quadrant in range(QUADRANTS):
+        first = QUADRANT * quadrant
+        q_rows = slice(SCALE_ROWS * quadrant, SCALE_ROWS * (quadrant + 1))
         nc.sync.dma_start(
-            out=plane[32 * quadrant : 32 * quadrant + 4, :, :].bitcast(I32),
-            in_=scales[:, 4 * quadrant : 4 * quadrant + 4, :].bitcast(I32).rearrange("g r n -> r g n"),
+            out=plane[first : first + SCALE_ROWS, :, :].bitcast(I32),
+            in_=scales[:, q_rows, :].bitcast(I32).rearrange("g r n -> r g n"),
         )
     return codes, plane
 
@@ -55,15 +61,15 @@ def tile_blockresmlp_mixerblock_pa_t_e_kernel(
         y_of, zT_of, zg_of, zq_of, acc1_of, v_of, gap_of, h_of = {}, {}, {}, {}, {}, {}, {}, {}
         hT_of, hg_of, hq_of, acc2_of, o_of = {}, {}, {}, {}, {}
 
-        def load_rows(k):
+        def load_rows(i):
             y_sb = rows_in.tile([P, LANES * FEAT], BF16)
-            nc.sync.dma_start(out=y_sb[:], in_=y_lanes[k * P : (k + 1) * P, :])
-            y_of[k] = y_sb
+            nc.sync.dma_start(out=y_sb[:], in_=y_lanes[i * P : (i + 1) * P, :])
+            y_of[i] = y_sb
 
         load_rows(0)
         w1_codes, w1_plane = load_weight(nc, const, w1_words, w1_scales, "w1")
-        for k in range(1, AHEAD):
-            load_rows(k)
+        for i in range(1, AHEAD):
+            load_rows(i)
         w2_codes, w2_plane = load_weight(nc, const, w2_words, w2_scales, "w2")
 
         identity = const.tile([P, P], F32)
@@ -92,26 +98,26 @@ def tile_blockresmlp_mixerblock_pa_t_e_kernel(
             )
             return codes, plane
 
-        def transpose_y(k):
-            y_words = y_of[k][:].bitcast(F32)
+        def transpose_y(i):
+            y_words = y_of[i][:].bitcast(F32)
             zT = psum.tile([P, PACK, P], F32, bufs=1)
             for t in range(PACK):
                 nc.tensor.transpose(zT[:, t, :], y_words[:, t:FEAT:PACK], identity[:])
-            zT_of[k] = zT
+            zT_of[i] = zT
 
-        def split_lanes(k):
+        def split_lanes(i):
             zg = work.tile([P, LANES, P, PACK], BF16, align_bytes=64)
             nc.scalar.copy(
-                out=zg[:], in_=zT_of[k][:].bitcast(BF16).rearrange("p t (b g) -> p g b t", g=LANES)
+                out=zg[:], in_=zT_of[i][:].bitcast(BF16).rearrange("p t (b g) -> p g b t", g=LANES)
             )
-            zg_of[k] = zg
+            zg_of[i] = zg
 
-        def quantise_z(k):
-            zq_of[k] = quantise(zg_of[k], "z")
+        def quantise_z(i):
+            zq_of[i] = quantise(zg_of[i], "z")
 
-        def first_matmul(k):
-            z_codes, z_plane = zq_of[k]
-            acc1_of[k] = []
+        def first_matmul(i):
+            z_codes, z_plane = zq_of[i]
+            acc1_of[i] = []
             for g in range(LANES):
                 rows = slice(g * P, (g + 1) * P)
                 acc1 = psum.tile([P, FEAT], F32)
@@ -124,70 +130,67 @@ def tile_blockresmlp_mixerblock_pa_t_e_kernel(
                     start=True,
                     stop=True,
                 )
-                acc1_of[k].append(acc1)
+                acc1_of[i].append(acc1)
 
-        def add_b1(k):
+        def add_b1(i):
             v = rows_f32.tile([P, LANES, FEAT], F32)
             for g in range(LANES):
                 nc.vector.tensor_tensor(
-                    out=v[:, g, :], in0=acc1_of[k][g][:], in1=b1_all[:, g, :], op=ALU.add
+                    out=v[:, g, :], in0=acc1_of[i][g][:], in1=b1_all[:, g, :], op=ALU.add
                 )
-            v_of[k] = v
+            v_of[i] = v
 
-        def elu_gap(k):
+        def elu_gap(i):
             gap = work.tile([P, LANES * FEAT], F32)
-            nc.scalar.activation(out=gap[:], in_=v_of[k][:].rearrange("p g n -> p (g n)"), func=ACT.Exp)
+            nc.scalar.activation(out=gap[:], in_=v_of[i][:].rearrange("p g n -> p (g n)"), func=ACT.Exp)
             nc.scalar.activation(out=gap[:], in_=gap[:], func=ACT.Relu, scale=-1.0, bias=1.0)
-            gap_of[k] = gap
+            gap_of[i] = gap
 
-        def elu_max(k):
+        def elu_max(i):
             h = work.tile([P, LANES * FEAT], BF16)
             nc.vector.scalar_tensor_tensor(
                 out=h[:],
-                in0=gap_of[k][:],
+                in0=gap_of[i][:],
                 scalar=-1.0,
-                in1=v_of[k][:].rearrange("p g n -> p (g n)"),
+                in1=v_of[i][:].rearrange("p g n -> p (g n)"),
                 op0=ALU.mult,
                 op1=ALU.max,
             )
-            h_of[k] = h
+            h_of[i] = h
 
-        def transpose_h(k):
-            h_words = h_of[k][:].bitcast(F32)
-            hT = psum.tile([P, LANES, 2, P], F32, bufs=1)
+        def transpose_h(i):
+            h_words = h_of[i][:].bitcast(F32)
+            lane_words = FEAT // 2
+            hT = psum.tile([P, LANES, PAIRS, P], F32, bufs=1)
             for g in range(LANES):
-                for u in range(2):
+                for u in range(PAIRS):
                     nc.tensor.transpose(
-                        hT[:, g, u, :], h_words[:, g * HALF + u : (g + 1) * HALF : 2], identity[:]
+                        hT[:, g, u, :],
+                        h_words[:, g * lane_words + u : (g + 1) * lane_words : PAIRS],
+                        identity[:],
                     )
-            hT_of[k] = hT
+            hT_of[i] = hT
 
-        def join_words(k):
+        def join_words(i):
             hg = work.tile([P, LANES, P, PACK], BF16, align_bytes=64)
-            nc.scalar.copy(out=hg[:].bitcast(F32), in_=hT_of[k][:].rearrange("p g u b -> p g b u"))
-            hg_of[k] = hg
+            nc.scalar.copy(out=hg[:].bitcast(F32), in_=hT_of[i][:].rearrange("p g u b -> p g b u"))
+            hg_of[i] = hg
 
-        def residual_and_bias(k):
-            o_sb = v_of[k][:].rearrange("p g n -> p (g n)")
-            width = LANES * FEAT // PIECES
-            for piece in range(PIECES):
-                cols = slice(piece * width, (piece + 1) * width)
-                nc.gpsimd.tensor_tensor(
-                    out=o_sb[:, cols],
-                    in0=y_of[k][:, cols],
-                    in1=b2_cols[:].rearrange("p d g -> p (d g)")[:, cols],
-                    op=ALU.add,
-                )
-            o_of[k] = o_sb
+        def residual_and_bias(i):
+            o_sb = v_of[i][:].rearrange("p g n -> p (g n)")
+            nc.gpsimd.tensor_tensor(
+                out=o_sb, in0=y_of[i][:], in1=b2_cols[:].rearrange("p d g -> p (d g)"), op=ALU.add
+            )
+            o_of[i] = o_sb
 
-        def quantise_h(k):
-            hq_of[k] = quantise(hg_of[k], "h")
+        def quantise_h(i):
+            hq_of[i] = quantise(hg_of[i], "h")
 
-        def second_matmul(k):
-            h_codes, h_plane = hq_of[k]
-            acc2_of[k] = []
-            for half in range(2):
-                cols = slice(half * HALF, (half + 1) * HALF)
+        def second_matmul(i):
+            h_codes, h_plane = hq_of[i]
+            acc2_of[i] = []
+            for half in range(HALVES):
+                feats = slice(half * HALF, (half + 1) * HALF)
                 acc2 = psum.tile([P, LANES, HALF], F32, bufs=4)
                 for g in range(LANES):
                     rows = slice(g * P, (g + 1) * P)
@@ -195,52 +198,53 @@ def tile_blockresmlp_mixerblock_pa_t_e_kernel(
                         out=acc2[:, g, :],
                         lhsT=h_codes[:, rows].bitcast(FP8X4),
                         lhsT_scale=h_plane[:, rows],
-                        rhs=w2_codes[:, g, cols].bitcast(FP8X4),
-                        rhs_scale=w2_plane[:, g, cols],
+                        rhs=w2_codes[:, g, feats].bitcast(FP8X4),
+                        rhs_scale=w2_plane[:, g, feats],
                         start=True,
                         stop=True,
                     )
-                acc2_of[k].append(acc2)
+                acc2_of[i].append(acc2)
 
-        def add_to_out_and_store(k):
-            for half in range(2):
-                o_cols = o_of[k][:, half * FEAT : (half + 1) * FEAT].rearrange("p (d g) -> p d g", g=LANES)
+        def add_to_out_and_store(i):
+            width = LANES * HALF
+            for half in range(HALVES):
+                o_cols = o_of[i][:, half * width : (half + 1) * width].rearrange("p (d g) -> p d g", g=LANES)
                 nc.vector.tensor_tensor(
-                    out=o_cols, in0=acc2_of[k][half][:].rearrange("p g d -> p d g"), in1=o_cols, op=ALU.add
+                    out=o_cols, in0=acc2_of[i][half][:].rearrange("p g d -> p d g"), in1=o_cols, op=ALU.add
                 )
-            nc.sync.dma_start(out=out[k * P : (k + 1) * P, :], in_=o_of[k][:])
+            nc.sync.dma_start(out=out[i * P : (i + 1) * P, :], in_=o_of[i][:])
 
-        def live(k):
-            return 0 <= k < N_TILES
+        def live(i):
+            return 0 <= i < N_TILES
 
         with tc.manual_schedule():
             for step in range(N_TILES + LAST_STAGE):
-                k0, k1, k2, k3 = step, step - 1, step - 2, step - 3
-                k4, k5, k6, k7 = step - 4, step - 5, step - 6, step - 7
-                if live(k0 + AHEAD):
-                    load_rows(k0 + AHEAD)
-                if live(k1):
-                    split_lanes(k1)
-                if live(k5):
-                    join_words(k5)
-                if live(k2):
-                    quantise_z(k2)
-                if live(k6):
-                    quantise_h(k6)
-                if live(k4):
-                    elu_max(k4)
-                    residual_and_bias(k4)
-                if live(k2):
-                    first_matmul(k2)
-                if live(k6):
-                    second_matmul(k6)
-                if live(k0):
-                    transpose_y(k0)
-                if live(k4):
-                    transpose_h(k4)
-                if live(k3):
-                    elu_gap(k3)
-                if live(k7):
-                    add_to_out_and_store(k7)
-                if live(k2):
-                    add_b1(k2)
+                i0, i1, i2, i3 = step, step - 1, step - 2, step - 3
+                i4, i5, i6, i7 = step - 4, step - 5, step - 6, step - 7
+                if live(i0 + AHEAD):
+                    load_rows(i0 + AHEAD)
+                if live(i1):
+                    split_lanes(i1)
+                if live(i5):
+                    join_words(i5)
+                if live(i2):
+                    quantise_z(i2)
+                if live(i6):
+                    quantise_h(i6)
+                if live(i4):
+                    elu_max(i4)
+                    residual_and_bias(i4)
+                if live(i2):
+                    first_matmul(i2)
+                if live(i6):
+                    second_matmul(i6)
+                if live(i0):
+                    transpose_y(i0)
+                if live(i4):
+                    transpose_h(i4)
+                if live(i3):
+                    elu_gap(i3)
+                if live(i7):
+                    add_to_out_and_store(i7)
+                if live(i2):
+                    add_b1(i2)

@@ -12,25 +12,24 @@ ALU = mybir.AluOpType
 
 P = 128
 PACK = 4
-PAIRS = PACK // 2
 LANES = 2
 ROWS = 4096
 FEAT = 512
-N_TILES = ROWS // P
-HALVES = 2
-HALF = FEAT // HALVES
+TILES = 2
+BLOCK = TILES * P
+N_BLOCKS = ROWS // BLOCK
+PAIRS = PACK // 2
 QUADRANTS = 4
 QUADRANT = P // QUADRANTS
 SCALE_ROWS = 4
-AHEAD = 4
-LAST_STAGE = 7
+AHEAD = 2
 
 FLOPS = 2 * 2 * LANES * ROWS * FEAT * FEAT
 
 
 def load_weight(nc, pool, words, scales, label):
-    codes = pool.tile([P, LANES, FEAT], U32, name=label + "_codes", align_bytes=64)
-    plane = pool.tile([P, LANES, FEAT], U8, name=label + "_plane", align_bytes=64)
+    codes = pool.tile([P, LANES, FEAT], U32, name=label + "_raw_codes", align_bytes=64)
+    plane = pool.tile([P, LANES, FEAT], U8, name=label + "_raw_plane", align_bytes=64)
     nc.vector.memset(plane[:].bitcast(I32), 0)
     nc.sync.dma_start(
         out=codes[:].bitcast(I32),
@@ -46,6 +45,29 @@ def load_weight(nc, pool, words, scales, label):
     return codes, plane
 
 
+def permute_columns(nc, pool, raw_codes, raw_plane, label):
+    codes = pool.tile([P, LANES, FEAT], U32, name=label + "_codes", align_bytes=64)
+    plane = pool.tile([P, LANES, FEAT], U8, name=label + "_plane", align_bytes=64)
+    for g in range(LANES):
+        nc.vector.tensor_copy(
+            out=codes[:, g, :].bitcast(I32).rearrange("p (t m) -> p t m", t=PACK),
+            in_=raw_codes[:, g, :].bitcast(I32).rearrange("p (m t) -> p t m", t=PACK),
+        )
+        nc.vector.tensor_copy(
+            out=plane[:, g, :].rearrange("p (t m) -> p t m", t=PACK),
+            in_=raw_plane[:, g, :].rearrange("p (m t) -> p t m", t=PACK),
+        )
+    return codes, plane
+
+
+def load_bias(nc, pool, bias, label):
+    raw = pool.tile([P, LANES, PACK], BF16, name=label + "_raw")
+    nc.scalar.dma_start(out=raw[:], in_=bias.rearrange("g o (p t) -> p (g o) t", t=PACK))
+    column = pool.tile([P, LANES, PACK], F32, name=label + "_column")
+    nc.vector.tensor_copy(out=column[:], in_=raw[:])
+    return column
+
+
 def tile_blockresmlp_mixerblock_pa_t_e_kernel(
     tc, y_lanes, w1_words, w1_scales, b1, w2_words, w2_scales, b2, out
 ):
@@ -53,198 +75,207 @@ def tile_blockresmlp_mixerblock_pa_t_e_kernel(
 
     with (
         tc.tile_pool(name="const", bufs=1) as const,
-        tc.tile_pool(name="rows_in", bufs=AHEAD + 5) as rows_in,
-        tc.tile_pool(name="rows_f32", bufs=8) as rows_f32,
+        tc.tile_pool(name="rows_in", bufs=TILES * (AHEAD + 2)) as rows_in,
+        tc.tile_pool(name="zpool", bufs=5) as zpool,
         tc.tile_pool(name="work", bufs=3) as work,
+        tc.tile_pool(name="rows_out", bufs=4) as rows_out,
         tc.psum_pool(name="psum", bufs=2) as psum,
     ):
-        y_of, zT_of, zg_of, zq_of, acc1_of, v_of, gap_of, h_of = {}, {}, {}, {}, {}, {}, {}, {}
-        hT_of, hg_of, hq_of, acc2_of, o_of = {}, {}, {}, {}, {}
+        y_of, zT_of, zg_of, zq_of, acc1_of, e_of, a_of = {}, {}, {}, {}, {}, {}, {}
+        hg_of, hq_of, acc2_of, r_of, oT_of, o_of = {}, {}, {}, {}, {}, {}
 
         def load_rows(i):
             y_sb = rows_in.tile([P, LANES * FEAT], BF16)
             nc.sync.dma_start(out=y_sb[:], in_=y_lanes[i * P : (i + 1) * P, :])
             y_of[i] = y_sb
 
-        load_rows(0)
-        w1_codes, w1_plane = load_weight(nc, const, w1_words, w1_scales, "w1")
-        for i in range(1, AHEAD):
-            load_rows(i)
-        w2_codes, w2_plane = load_weight(nc, const, w2_words, w2_scales, "w2")
+        def load_block(k):
+            for j in range(TILES):
+                load_rows(k * TILES + j)
+
+        load_block(0)
+        raw1 = load_weight(nc, const, w1_words, w1_scales, "w1")
+        load_block(1)
+        raw2 = load_weight(nc, const, w2_words, w2_scales, "w2")
+        b1_col = load_bias(nc, const, b1, "b1")
+        b2_col = load_bias(nc, const, b2, "b2")
 
         identity = const.tile([P, P], F32)
         make_identity(nc, identity[:])
 
-        b1_all = const.tile([P, LANES, FEAT], BF16)
-        nc.scalar.dma_start(
-            out=b1_all[:].rearrange("p g n -> p (g n)"),
-            in_=b1.rearrange("g o n -> (g o n)").partition_broadcast(P),
-        )
-        b2_all = const.tile([P, LANES, FEAT], BF16)
-        nc.scalar.dma_start(
-            out=b2_all[:].rearrange("p g d -> p (g d)"),
-            in_=b2.rearrange("g o d -> (g o d)").partition_broadcast(P),
-        )
-        b2_cols = const.tile([P, FEAT, LANES], BF16)
-        nc.vector.tensor_copy(out=b2_cols[:], in_=b2_all[:].rearrange("p g d -> p d g"))
+        w1_codes, w1_plane = permute_columns(nc, const, raw1[0], raw1[1], "w1")
 
-        def quantise(grouped, label):
-            codes = work.tile([P, LANES * P], U32, name=label + "_codes", align_bytes=64)
-            plane = work.tile([P, LANES * P], U8, name=label + "_plane", align_bytes=64)
-            nc.vector.quantize_mx(
-                out=codes[:].bitcast(FP8X4),
-                scales=plane[:],
-                in_=grouped[:].rearrange("p g b t -> p (g b t)"),
-            )
+        def quantise(grouped, width, label):
+            codes = work.tile([P, width], U32, name=label + "_codes", align_bytes=64)
+            plane = work.tile([P, width], U8, name=label + "_plane", align_bytes=64)
+            nc.vector.quantize_mx(out=codes[:].bitcast(FP8X4), scales=plane[:], in_=grouped)
             return codes, plane
 
-        def transpose_y(i):
+        def transpose_y(k, j):
+            i = k * TILES + j
             y_words = y_of[i][:].bitcast(F32)
-            zT = psum.tile([P, PACK, P], F32, bufs=1)
+            zT = psum.tile([P, PACK, P], F32)
             for t in range(PACK):
                 nc.tensor.transpose(zT[:, t, :], y_words[:, t:FEAT:PACK], identity[:])
             zT_of[i] = zT
 
-        def split_lanes(i):
-            zg = work.tile([P, LANES, P, PACK], BF16, align_bytes=64)
-            nc.scalar.copy(
-                out=zg[:], in_=zT_of[i][:].bitcast(BF16).rearrange("p t (b g) -> p g b t", g=LANES)
+        def split_lanes(k, j, copy):
+            if j == 0:
+                zg = zpool.tile([P, LANES, BLOCK, PACK], BF16, align_bytes=64)
+                zg_of[k] = zg
+            copy(
+                out=zg_of[k][:, :, j * P : (j + 1) * P, :],
+                in_=zT_of[k * TILES + j][:].bitcast(BF16).rearrange("p t (b g) -> p g b t", g=LANES),
             )
-            zg_of[i] = zg
 
-        def quantise_z(i):
-            zq_of[i] = quantise(zg_of[i], "z")
+        def quantise_z(k):
+            zq_of[k] = quantise(zg_of[k][:].rearrange("p g b t -> p (g b t)"), LANES * BLOCK, "z")
 
-        def first_matmul(i):
-            z_codes, z_plane = zq_of[i]
-            acc1_of[i] = []
-            for g in range(LANES):
-                rows = slice(g * P, (g + 1) * P)
-                acc1 = psum.tile([P, FEAT], F32)
+        def first_matmul(k, g, pair):
+            codes, plane = zq_of[k]
+            rows = slice(g * BLOCK, (g + 1) * BLOCK)
+            acc1 = psum.tile([P, PAIRS, BLOCK], F32)
+            for s in range(PAIRS):
+                t = pair * PAIRS + s
+                cols = slice(t * P, (t + 1) * P)
                 nc.tensor.matmul_mx(
-                    out=acc1[:],
-                    lhsT=z_codes[:, rows].bitcast(FP8X4),
-                    lhsT_scale=z_plane[:, rows],
-                    rhs=w1_codes[:, g, :].bitcast(FP8X4),
-                    rhs_scale=w1_plane[:, g, :],
+                    out=acc1[:, s, :],
+                    lhsT=w1_codes[:, g, cols].bitcast(FP8X4),
+                    lhsT_scale=w1_plane[:, g, cols],
+                    rhs=codes[:, rows].bitcast(FP8X4),
+                    rhs_scale=plane[:, rows],
                     start=True,
                     stop=True,
                 )
-                acc1_of[i].append(acc1)
+            acc1_of[k, g, pair] = acc1
 
-        def add_b1(i):
-            v = rows_f32.tile([P, LANES, FEAT], F32)
-            for g in range(LANES):
-                nc.vector.tensor_tensor(
-                    out=v[:, g, :], in0=acc1_of[i][g][:], in1=b1_all[:, g, :], op=ALU.add
+        def elu_parts(k, g, pair):
+            if pair == 0:
+                e = work.tile([P, PACK, BLOCK], F32)
+                a = work.tile([P, PACK, BLOCK], BF16)
+                e_of[k, g], a_of[k, g] = e, a
+            acc1 = acc1_of[k, g, pair]
+            for s in range(PAIRS):
+                t = pair * PAIRS + s
+                nc.scalar.activation(
+                    out=e_of[k, g][:, t, :], in_=acc1[:, s, :], func=ACT.Exp, bias=b1_col[:, g, t : t + 1]
                 )
-            v_of[i] = v
+            for s in range(PAIRS):
+                t = pair * PAIRS + s
+                nc.scalar.activation(
+                    out=a_of[k, g][:, t, :], in_=acc1[:, s, :], func=ACT.Relu, bias=b1_col[:, g, t : t + 1]
+                )
 
-        def elu_gap(i):
-            gap = work.tile([P, LANES * FEAT], F32)
-            nc.scalar.activation(out=gap[:], in_=v_of[i][:].rearrange("p g n -> p (g n)"), func=ACT.Exp)
-            nc.scalar.activation(out=gap[:], in_=gap[:], func=ACT.Relu, scale=-1.0, bias=1.0)
-            gap_of[i] = gap
-
-        def elu_max(i):
-            h = work.tile([P, LANES * FEAT], BF16)
+        def elu_join(k, g):
+            hg = work.tile([P, BLOCK, PACK], BF16, align_bytes=64)
             nc.vector.scalar_tensor_tensor(
-                out=h[:],
-                in0=gap_of[i][:],
+                out=hg[:],
+                in0=e_of[k, g][:].rearrange("p t b -> p b t"),
                 scalar=-1.0,
-                in1=v_of[i][:].rearrange("p g n -> p (g n)"),
-                op0=ALU.mult,
-                op1=ALU.max,
+                in1=a_of[k, g][:].rearrange("p t b -> p b t"),
+                op0=ALU.add,
+                op1=ALU.min,
             )
-            h_of[i] = h
+            hg_of[k, g] = hg
 
-        def transpose_h(i):
-            h_words = h_of[i][:].bitcast(F32)
-            lane_words = FEAT // 2
-            hT = psum.tile([P, LANES, PAIRS, P], F32, bufs=1)
-            for g in range(LANES):
-                for u in range(PAIRS):
-                    nc.tensor.transpose(
-                        hT[:, g, u, :],
-                        h_words[:, g * lane_words + u : (g + 1) * lane_words : PAIRS],
-                        identity[:],
-                    )
-            hT_of[i] = hT
+        def quantise_h(k, g):
+            hq_of[k, g] = quantise(hg_of[k, g][:].rearrange("p b t -> p (b t)"), BLOCK, "h")
 
-        def join_words(i):
-            hg = work.tile([P, LANES, P, PACK], BF16, align_bytes=64)
-            nc.scalar.copy(out=hg[:].bitcast(F32), in_=hT_of[i][:].rearrange("p g u b -> p g b u"))
-            hg_of[i] = hg
-
-        def residual_and_bias(i):
-            o_sb = v_of[i][:].rearrange("p g n -> p (g n)")
-            nc.gpsimd.tensor_tensor(
-                out=o_sb, in0=y_of[i][:], in1=b2_cols[:].rearrange("p d g -> p (d g)"), op=ALU.add
-            )
-            o_of[i] = o_sb
-
-        def quantise_h(i):
-            hq_of[i] = quantise(hg_of[i], "h")
-
-        def second_matmul(i):
-            h_codes, h_plane = hq_of[i]
-            acc2_of[i] = []
-            for half in range(HALVES):
-                feats = slice(half * HALF, (half + 1) * HALF)
-                acc2 = psum.tile([P, LANES, HALF], F32, bufs=4)
-                for g in range(LANES):
-                    rows = slice(g * P, (g + 1) * P)
-                    nc.tensor.matmul_mx(
-                        out=acc2[:, g, :],
-                        lhsT=h_codes[:, rows].bitcast(FP8X4),
-                        lhsT_scale=h_plane[:, rows],
-                        rhs=w2_codes[:, g, feats].bitcast(FP8X4),
-                        rhs_scale=w2_plane[:, g, feats],
-                        start=True,
-                        stop=True,
-                    )
-                acc2_of[i].append(acc2)
-
-        def add_to_out_and_store(i):
-            width = LANES * HALF
-            for half in range(HALVES):
-                o_cols = o_of[i][:, half * width : (half + 1) * width].rearrange("p (d g) -> p d g", g=LANES)
-                nc.vector.tensor_tensor(
-                    out=o_cols, in0=acc2_of[i][half][:].rearrange("p g d -> p d g"), in1=o_cols, op=ALU.add
+        def second_matmul(k, g, pair):
+            codes, plane = hq_of[k, g]
+            acc2 = psum.tile([P, PAIRS, BLOCK], F32)
+            for s in range(PAIRS):
+                t = pair * PAIRS + s
+                cols = slice(t * P, (t + 1) * P)
+                nc.tensor.matmul_mx(
+                    out=acc2[:, s, :],
+                    lhsT=w2_codes[:, g, cols].bitcast(FP8X4),
+                    lhsT_scale=w2_plane[:, g, cols],
+                    rhs=codes[:].bitcast(FP8X4),
+                    rhs_scale=plane[:],
+                    start=True,
+                    stop=True,
                 )
-            nc.sync.dma_start(out=out[i * P : (i + 1) * P, :], in_=o_of[i][:])
+            acc2_of[k, g, pair] = acc2
 
-        def live(i):
-            return 0 <= i < N_TILES
+        def add_residual(k, g, pair):
+            if (g, pair) == (0, 0):
+                r = work.tile([P, LANES, PACK, BLOCK], F32, bufs=2)
+                r_of[k] = r
+            for s in range(PAIRS):
+                t = pair * PAIRS + s
+                nc.vector.scalar_tensor_tensor(
+                    out=r_of[k][:, g, t, :],
+                    in0=acc2_of[k, g, pair][:, s, :],
+                    scalar=b2_col[:, g, t : t + 1],
+                    in1=zg_of[k][:, g, :, t],
+                    op0=ALU.add,
+                    op1=ALU.add,
+                )
+
+        def transpose_out(k, j, pair):
+            oT = psum.tile([P, PAIRS, LANES, P], F32)
+            for s in range(PAIRS):
+                for g in range(LANES):
+                    nc.tensor.transpose(
+                        oT[:, s, g, :], r_of[k][:, g, pair * PAIRS + s, j * P : (j + 1) * P], identity[:]
+                    )
+            oT_of[k, j, pair] = oT
+
+        def copy_out(k, j, pair, copy):
+            if pair == 0:
+                o_sb = rows_out.tile([P, P, PAIRS, PAIRS * LANES], F32)
+                o_of[k, j] = o_sb
+            copy(
+                out=o_of[k, j][:, :, pair, :],
+                in_=oT_of[k, j, pair][:].rearrange("b s g p -> b p (s g)"),
+            )
+
+        def store(k, j):
+            i = k * TILES + j
+            nc.sync.dma_start(
+                out=out[i * P : (i + 1) * P, :], in_=o_of[k, j][:].rearrange("b p u c -> b (p u c)")
+            )
+
+        def live(k):
+            return 0 <= k < N_BLOCKS
+
+        scalar_copy, vector_copy = nc.scalar.copy, nc.vector.tensor_copy
 
         with tc.manual_schedule():
-            for step in range(N_TILES + LAST_STAGE):
-                i0, i1, i2, i3 = step, step - 1, step - 2, step - 3
-                i4, i5, i6, i7 = step - 4, step - 5, step - 6, step - 7
-                if live(i0 + AHEAD):
-                    load_rows(i0 + AHEAD)
-                if live(i1):
-                    split_lanes(i1)
-                if live(i5):
-                    join_words(i5)
-                if live(i2):
-                    quantise_z(i2)
-                if live(i6):
-                    quantise_h(i6)
-                if live(i4):
-                    elu_max(i4)
-                    residual_and_bias(i4)
-                if live(i2):
-                    first_matmul(i2)
-                if live(i6):
-                    second_matmul(i6)
-                if live(i0):
-                    transpose_y(i0)
-                if live(i4):
-                    transpose_h(i4)
-                if live(i3):
-                    elu_gap(i3)
-                if live(i7):
-                    add_to_out_and_store(i7)
-                if live(i2):
-                    add_b1(i2)
+            for k in range(-2, N_BLOCKS + 2):
+                if k == 0:
+                    w2_codes, w2_plane = permute_columns(nc, const, raw2[0], raw2[1], "w2")
+                if live(k + 2 + AHEAD):
+                    load_block(k + 2 + AHEAD)
+                for q in range(4):
+                    g, pair = divmod(q, PAIRS)
+                    j, opair = divmod(q, PAIRS)
+                    if live(k):
+                        first_matmul(k, g, pair)
+                    if live(k - 1):
+                        second_matmul(k - 1, g, pair)
+                    if live(k - 2):
+                        transpose_out(k - 2, j, opair)
+                    if live(k + 2) and pair == 0:
+                        transpose_y(k + 2, g)
+                    if live(k):
+                        elu_parts(k, g, pair)
+                    if pair == 0:
+                        kk, gg = (k - 1, 1) if g == 0 else (k, 0)
+                        if live(kk):
+                            elu_join(kk, gg)
+                    if live(k - 1):
+                        add_residual(k - 1, g, pair)
+                    if pair == 1:
+                        kk, gg = (k - 1, 1) if g == 0 else (k, 0)
+                        if live(kk):
+                            quantise_h(kk, gg)
+                    if q == 1 and live(k + 1):
+                        quantise_z(k + 1)
+                    if live(k + 2) and pair == 0:
+                        split_lanes(k + 2, g, scalar_copy)
+                    if live(k - 2):
+                        copy_out(k - 2, j, opair, scalar_copy if q == 1 else vector_copy)
+                        if opair == 1:
+                            store(k - 2, j)

@@ -15,14 +15,17 @@ PACK = 4
 LANES = 2
 ROWS = 4096
 FEAT = 512
-TILES = 2
-BLOCK = TILES * P
-N_BLOCKS = ROWS // BLOCK
+BLOCKS = [1] + [2] * 15 + [1]
+N_BLOCKS = len(BLOCKS)
+FIRST = [sum(BLOCKS[:k]) for k in range(N_BLOCKS)]
+N_TILES = ROWS // P
 PAIRS = PACK // 2
 QUADRANTS = 4
 QUADRANT = P // QUADRANTS
 SCALE_ROWS = 4
-AHEAD = 2
+LOAD_AHEAD = 6
+PREP_AHEAD = 3
+GROUP = 2
 
 FLOPS = 2 * 2 * LANES * ROWS * FEAT * FEAT
 
@@ -30,7 +33,7 @@ FLOPS = 2 * 2 * LANES * ROWS * FEAT * FEAT
 def load_weight(nc, pool, words, scales, label):
     codes = pool.tile([P, LANES, FEAT], U32, name=label + "_raw_codes", align_bytes=64)
     plane = pool.tile([P, LANES, FEAT], U8, name=label + "_raw_plane", align_bytes=64)
-    nc.vector.memset(plane[:].bitcast(I32), 0)
+    nc.gpsimd.memset(plane[:].bitcast(I32), 0)
     nc.sync.dma_start(
         out=codes[:].bitcast(I32),
         in_=words.rearrange("g p n t -> p g (n t)").bitcast(I32),
@@ -45,19 +48,15 @@ def load_weight(nc, pool, words, scales, label):
     return codes, plane
 
 
-def permute_columns(nc, pool, raw_codes, raw_plane, label):
-    codes = pool.tile([P, LANES, FEAT], U32, name=label + "_codes", align_bytes=64)
-    plane = pool.tile([P, LANES, FEAT], U8, name=label + "_plane", align_bytes=64)
-    for g in range(LANES):
-        nc.vector.tensor_copy(
-            out=codes[:, g, :].bitcast(I32).rearrange("p (t m) -> p t m", t=PACK),
-            in_=raw_codes[:, g, :].bitcast(I32).rearrange("p (m t) -> p t m", t=PACK),
-        )
-        nc.vector.tensor_copy(
-            out=plane[:, g, :].rearrange("p (t m) -> p t m", t=PACK),
-            in_=raw_plane[:, g, :].rearrange("p (m t) -> p t m", t=PACK),
-        )
-    return codes, plane
+def permute_columns(nc, codes, plane, raw_codes, raw_plane, g):
+    nc.vector.tensor_copy(
+        out=codes[:, g, :].bitcast(I32).rearrange("p (t m) -> p t m", t=PACK),
+        in_=raw_codes[:, g, :].bitcast(I32).rearrange("p (m t) -> p t m", t=PACK),
+    )
+    nc.vector.tensor_copy(
+        out=plane[:, g, :].rearrange("p (t m) -> p t m", t=PACK),
+        in_=raw_plane[:, g, :].rearrange("p (m t) -> p t m", t=PACK),
+    )
 
 
 def load_bias(nc, pool, bias, label):
@@ -75,9 +74,9 @@ def tile_blockresmlp_mixerblock_pa_t_e_kernel(
 
     with (
         tc.tile_pool(name="const", bufs=1) as const,
-        tc.tile_pool(name="rows_in", bufs=TILES * (AHEAD + 2)) as rows_in,
-        tc.tile_pool(name="zpool", bufs=5) as zpool,
-        tc.tile_pool(name="work", bufs=3) as work,
+        tc.tile_pool(name="rows_in", bufs=LOAD_AHEAD + 2) as rows_in,
+        tc.tile_pool(name="zpool", bufs=6) as zpool,
+        tc.tile_pool(name="work", bufs=4) as work,
         tc.tile_pool(name="rows_out", bufs=4) as rows_out,
         tc.psum_pool(name="psum", bufs=2) as psum,
     ):
@@ -89,21 +88,21 @@ def tile_blockresmlp_mixerblock_pa_t_e_kernel(
             nc.sync.dma_start(out=y_sb[:], in_=y_lanes[i * P : (i + 1) * P, :])
             y_of[i] = y_sb
 
-        def load_block(k):
-            for j in range(TILES):
-                load_rows(k * TILES + j)
-
-        load_block(0)
+        load_rows(0)
         raw1 = load_weight(nc, const, w1_words, w1_scales, "w1")
-        load_block(1)
+        for i in range(1, LOAD_AHEAD):
+            load_rows(i)
         raw2 = load_weight(nc, const, w2_words, w2_scales, "w2")
         b1_col = load_bias(nc, const, b1, "b1")
         b2_col = load_bias(nc, const, b2, "b2")
 
+        w1_codes = const.tile([P, LANES, FEAT], U32, align_bytes=64)
+        w1_plane = const.tile([P, LANES, FEAT], U8, align_bytes=64)
+        w2_codes = const.tile([P, LANES, FEAT], U32, align_bytes=64)
+        w2_plane = const.tile([P, LANES, FEAT], U8, align_bytes=64)
+
         identity = const.tile([P, P], F32)
         make_identity(nc, identity[:])
-
-        w1_codes, w1_plane = permute_columns(nc, const, raw1[0], raw1[1], "w1")
 
         def quantise(grouped, width, label):
             codes = work.tile([P, width], U32, name=label + "_codes", align_bytes=64)
@@ -111,32 +110,39 @@ def tile_blockresmlp_mixerblock_pa_t_e_kernel(
             nc.vector.quantize_mx(out=codes[:].bitcast(FP8X4), scales=plane[:], in_=grouped)
             return codes, plane
 
-        def transpose_y(k, j):
-            i = k * TILES + j
+        def rows_of(k):
+            return BLOCKS[k] * P
+
+        def ts_of(k, bank):
+            n = PACK // BLOCKS[k]
+            return range(bank * n, (bank + 1) * n)
+
+        def transpose_y(i):
             y_words = y_of[i][:].bitcast(F32)
-            zT = psum.tile([P, PACK, P], F32)
+            zT = psum.tile([P, PACK, P], F32, bufs=1)
             for t in range(PACK):
                 nc.tensor.transpose(zT[:, t, :], y_words[:, t:FEAT:PACK], identity[:])
             zT_of[i] = zT
 
-        def split_lanes(k, j, copy):
-            if j == 0:
-                zg = zpool.tile([P, LANES, BLOCK, PACK], BF16, align_bytes=64)
+        def split_lanes(i, lanes, copy):
+            k = block_of[i]
+            j = i - FIRST[k]
+            if k not in zg_of:
+                zg = zpool.tile([P, LANES, rows_of(k), PACK], BF16, align_bytes=64)
                 zg_of[k] = zg
             copy(
-                out=zg_of[k][:, :, j * P : (j + 1) * P, :],
-                in_=zT_of[k * TILES + j][:].bitcast(BF16).rearrange("p t (b g) -> p g b t", g=LANES),
+                out=zg_of[k][:, lanes, j * P : (j + 1) * P, :],
+                in_=zT_of[i][:].bitcast(BF16).rearrange("p t (b g) -> p g b t", g=LANES)[:, lanes],
             )
 
         def quantise_z(k):
-            zq_of[k] = quantise(zg_of[k][:].rearrange("p g b t -> p (g b t)"), LANES * BLOCK, "z")
+            zq_of[k] = quantise(zg_of[k][:].rearrange("p g b t -> p (g b t)"), LANES * rows_of(k), "z")
 
-        def first_matmul(k, g, pair):
+        def first_matmul(k, g, bank):
             codes, plane = zq_of[k]
-            rows = slice(g * BLOCK, (g + 1) * BLOCK)
-            acc1 = psum.tile([P, PAIRS, BLOCK], F32)
-            for s in range(PAIRS):
-                t = pair * PAIRS + s
+            rows = slice(g * rows_of(k), (g + 1) * rows_of(k))
+            acc1 = psum.tile([P, PACK // BLOCKS[k], rows_of(k)], F32, bufs=3)
+            for s, t in enumerate(ts_of(k, bank)):
                 cols = slice(t * P, (t + 1) * P)
                 nc.tensor.matmul_mx(
                     out=acc1[:, s, :],
@@ -147,27 +153,20 @@ def tile_blockresmlp_mixerblock_pa_t_e_kernel(
                     start=True,
                     stop=True,
                 )
-            acc1_of[k, g, pair] = acc1
+            acc1_of[k, g, bank] = acc1
 
-        def elu_parts(k, g, pair):
-            if pair == 0:
-                e = work.tile([P, PACK, BLOCK], F32)
-                a = work.tile([P, PACK, BLOCK], BF16)
+        def elu_parts(k, g, bank):
+            if bank == 0:
+                e = work.tile([P, PACK, rows_of(k)], F32)
+                a = work.tile([P, PACK, rows_of(k)], BF16)
                 e_of[k, g], a_of[k, g] = e, a
-            acc1 = acc1_of[k, g, pair]
-            for s in range(PAIRS):
-                t = pair * PAIRS + s
-                nc.scalar.activation(
-                    out=e_of[k, g][:, t, :], in_=acc1[:, s, :], func=ACT.Exp, bias=b1_col[:, g, t : t + 1]
-                )
-            for s in range(PAIRS):
-                t = pair * PAIRS + s
-                nc.scalar.activation(
-                    out=a_of[k, g][:, t, :], in_=acc1[:, s, :], func=ACT.Relu, bias=b1_col[:, g, t : t + 1]
-                )
+            acc1 = acc1_of[k, g, bank]
+            for func, part in ((ACT.Exp, e_of[k, g]), (ACT.Relu, a_of[k, g])):
+                for s, t in enumerate(ts_of(k, bank)):
+                    nc.scalar.activation(out=part[:, t, :], in_=acc1[:, s, :], func=func, bias=b1_col[:, g, t : t + 1])
 
         def elu_join(k, g):
-            hg = work.tile([P, BLOCK, PACK], BF16, align_bytes=64)
+            hg = work.tile([P, rows_of(k), PACK], BF16, align_bytes=64)
             nc.vector.scalar_tensor_tensor(
                 out=hg[:],
                 in0=e_of[k, g][:].rearrange("p t b -> p b t"),
@@ -179,13 +178,12 @@ def tile_blockresmlp_mixerblock_pa_t_e_kernel(
             hg_of[k, g] = hg
 
         def quantise_h(k, g):
-            hq_of[k, g] = quantise(hg_of[k, g][:].rearrange("p b t -> p (b t)"), BLOCK, "h")
+            hq_of[k, g] = quantise(hg_of[k, g][:].rearrange("p b t -> p (b t)"), rows_of(k), "h")
 
-        def second_matmul(k, g, pair):
+        def second_matmul(k, g, bank):
             codes, plane = hq_of[k, g]
-            acc2 = psum.tile([P, PAIRS, BLOCK], F32)
-            for s in range(PAIRS):
-                t = pair * PAIRS + s
+            acc2 = psum.tile([P, PACK // BLOCKS[k], rows_of(k)], F32)
+            for s, t in enumerate(ts_of(k, bank)):
                 cols = slice(t * P, (t + 1) * P)
                 nc.tensor.matmul_mx(
                     out=acc2[:, s, :],
@@ -196,17 +194,16 @@ def tile_blockresmlp_mixerblock_pa_t_e_kernel(
                     start=True,
                     stop=True,
                 )
-            acc2_of[k, g, pair] = acc2
+            acc2_of[k, g, bank] = acc2
 
-        def add_residual(k, g, pair):
-            if (g, pair) == (0, 0):
-                r = work.tile([P, LANES, PACK, BLOCK], F32, bufs=2)
+        def add_residual(k, g, bank):
+            if (g, bank) == (0, 0):
+                r = work.tile([P, LANES, PACK, rows_of(k)], F32, bufs=2)
                 r_of[k] = r
-            for s in range(PAIRS):
-                t = pair * PAIRS + s
+            for s, t in enumerate(ts_of(k, bank)):
                 nc.vector.scalar_tensor_tensor(
                     out=r_of[k][:, g, t, :],
-                    in0=acc2_of[k, g, pair][:, s, :],
+                    in0=acc2_of[k, g, bank][:, s, :],
                     scalar=b2_col[:, g, t : t + 1],
                     in1=zg_of[k][:, g, :, t],
                     op0=ALU.add,
@@ -223,7 +220,7 @@ def tile_blockresmlp_mixerblock_pa_t_e_kernel(
             oT_of[k, j, pair] = oT
 
         def copy_out(k, j, pair, copy):
-            if pair == 0:
+            if (k, j) not in o_of:
                 o_sb = rows_out.tile([P, P, PAIRS, PAIRS * LANES], F32)
                 o_of[k, j] = o_sb
             copy(
@@ -232,50 +229,89 @@ def tile_blockresmlp_mixerblock_pa_t_e_kernel(
             )
 
         def store(k, j):
-            i = k * TILES + j
+            i = FIRST[k] + j
             nc.sync.dma_start(
                 out=out[i * P : (i + 1) * P, :], in_=o_of[k, j][:].rearrange("b p u c -> b (p u c)")
             )
 
-        def live(k):
-            return 0 <= k < N_BLOCKS
-
         scalar_copy, vector_copy = nc.scalar.copy, nc.vector.tensor_copy
 
+        blocks = range(N_BLOCKS)
+        block_of = [k for k in blocks for j in range(BLOCKS[k])]
+        units = [(k, g, bank) for k in blocks for g in range(LANES) for bank in range(BLOCKS[k])]
+        out_banks = [(k, j, pair) for k in blocks for pair in range(PAIRS) for j in range(BLOCKS[k])]
+        steps = len(units)
+        both = slice(0, LANES)
+        joined, quantised, added = [], {}, {}
+        n_first = n_second = n_out = n_zq = 0
+        n_tiles = 2
+        n_loaded = LOAD_AHEAD
+
+        def parts(k, j, pair):
+            n = PACK // BLOCKS[k]
+            return {(k, g, t // n) for g in range(LANES) for t in range(pair * PAIRS, (pair + 1) * PAIRS)}
+
         with tc.manual_schedule():
-            for k in range(-2, N_BLOCKS + 2):
-                if k == 0:
-                    w2_codes, w2_plane = permute_columns(nc, const, raw2[0], raw2[1], "w2")
-                if live(k + 2 + AHEAD):
-                    load_block(k + 2 + AHEAD)
-                for q in range(4):
-                    g, pair = divmod(q, PAIRS)
-                    j, opair = divmod(q, PAIRS)
-                    if live(k):
-                        first_matmul(k, g, pair)
-                    if live(k - 1):
-                        second_matmul(k - 1, g, pair)
-                    if live(k - 2):
-                        transpose_out(k - 2, j, opair)
-                    if live(k + 2) and pair == 0:
-                        transpose_y(k + 2, g)
-                    if live(k):
-                        elu_parts(k, g, pair)
-                    if pair == 0:
-                        kk, gg = (k - 1, 1) if g == 0 else (k, 0)
-                        if live(kk):
-                            elu_join(kk, gg)
-                    if live(k - 1):
-                        add_residual(k - 1, g, pair)
+            transpose_y(0)
+            split_lanes(0, both, scalar_copy)
+            permute_columns(nc, w1_codes, w1_plane, raw1[0], raw1[1], 0)
+            quantise_z(0)
+            permute_columns(nc, w1_codes, w1_plane, raw1[0], raw1[1], 1)
+            transpose_y(1)
+            split_lanes(1, both, vector_copy)
+            n_zq = 1
+            step = 0
+            while n_out < len(out_banks):
+                draining = n_first >= steps
+                group = GROUP if 2 <= n_first < steps - 4 else 1
+                take = units[n_first : n_first + group]
+                n_first += len(take)
+                prep = range(n_tiles, min(N_TILES, n_first // 2 + PREP_AHEAD))
+                n_tiles += len(prep)
+                for i in prep:
+                    if n_loaded < N_TILES:
+                        load_rows(n_loaded)
+                        n_loaded += 1
+                ending = n_first > steps - 4
+                seconds = [n for n in range(n_second, min(n_second + (GROUP if ending else group), steps)) if quantised.get(units[n][:2], step) < step]
+                n_second += len(seconds)
+                outs = []
+                while (
+                    n_out < len(out_banks)
+                    and len(outs) < (GROUP if ending else group)
+                    and all(added.get(part, step) < step for part in parts(*out_banks[n_out]))
+                ):
+                    outs.append(out_banks[n_out])
+                    n_out += 1
+                for unit in take:
+                    first_matmul(*unit)
+                for n in seconds:
+                    second_matmul(*units[n])
+                for bank in outs:
+                    transpose_out(*bank)
+                for i in prep:
+                    transpose_y(i)
+                if n_zq < N_BLOCKS and FIRST[n_zq] + BLOCKS[n_zq] <= n_tiles - len(prep):
+                    quantise_z(n_zq)
+                    n_zq += 1
+                for k, g in joined:
+                    elu_join(k, g)
+                if 1 <= step <= LANES:
+                    permute_columns(nc, w2_codes, w2_plane, raw2[0], raw2[1], step - 1)
+                for n in seconds:
+                    add_residual(*units[n])
+                    added[units[n]] = step
+                for k, g in joined:
+                    quantise_h(k, g)
+                    quantised[k, g] = step
+                joined = [unit[:2] for unit in take if unit[2] == BLOCKS[unit[0]] - 1]
+                for unit in take:
+                    elu_parts(*unit)
+                for i in prep:
+                    split_lanes(i, both, scalar_copy)
+                for n, (k, j, pair) in enumerate(outs):
+                    on_scalar = (n == 0) if draining else (n % 2 == 1)
+                    copy_out(k, j, pair, scalar_copy if on_scalar else vector_copy)
                     if pair == 1:
-                        kk, gg = (k - 1, 1) if g == 0 else (k, 0)
-                        if live(kk):
-                            quantise_h(kk, gg)
-                    if q == 1 and live(k + 1):
-                        quantise_z(k + 1)
-                    if live(k + 2) and pair == 0:
-                        split_lanes(k + 2, g, scalar_copy)
-                    if live(k - 2):
-                        copy_out(k - 2, j, opair, scalar_copy if q == 1 else vector_copy)
-                        if opair == 1:
-                            store(k - 2, j)
+                        store(k, j)
+                step += 1

@@ -90,9 +90,11 @@ def tile_blockresmlp_mixerblock_pa_t_e_kernel(
 
         load_rows(0)
         raw1 = load_weight(nc, const, w1_words, w1_scales, "w1")
-        for i in range(1, LOAD_AHEAD):
+        for i in range(1, 3):
             load_rows(i)
         raw2 = load_weight(nc, const, w2_words, w2_scales, "w2")
+        for i in range(3, LOAD_AHEAD):
+            load_rows(i)
         b1_col = load_bias(nc, const, b1, "b1")
         b2_col = load_bias(nc, const, b2, "b2")
 
@@ -243,7 +245,7 @@ def tile_blockresmlp_mixerblock_pa_t_e_kernel(
         steps = len(units)
         both = slice(0, LANES)
         joined, quantised, added = [], {}, {}
-        n_first = n_second = n_out = n_zq = 0
+        n_first = n_second = n_out = n_copied = n_zq = 0
         n_tiles = 2
         n_loaded = LOAD_AHEAD
 
@@ -291,13 +293,13 @@ def tile_blockresmlp_mixerblock_pa_t_e_kernel(
                     transpose_out(*bank)
                 for i in prep:
                     transpose_y(i)
+                if step < LANES:
+                    permute_columns(nc, w2_codes, w2_plane, raw2[0], raw2[1], step)
                 if n_zq < N_BLOCKS and FIRST[n_zq] + BLOCKS[n_zq] <= n_tiles - len(prep):
                     quantise_z(n_zq)
                     n_zq += 1
                 for k, g in joined:
                     elu_join(k, g)
-                if 1 <= step <= LANES:
-                    permute_columns(nc, w2_codes, w2_plane, raw2[0], raw2[1], step - 1)
                 for n in seconds:
                     add_residual(*units[n])
                     added[units[n]] = step
@@ -310,7 +312,8 @@ def tile_blockresmlp_mixerblock_pa_t_e_kernel(
                 for i in prep:
                     split_lanes(i, both, scalar_copy)
                 for n, (k, j, pair) in enumerate(outs):
-                    on_scalar = (n == 0) if draining else (n % 2 == 1)
+                    n_copied += 1
+                    on_scalar = (n == 0) if draining else n_copied % 8 in (0, 2, 5)
                     copy_out(k, j, pair, scalar_copy if on_scalar else vector_copy)
                     if pair == 1:
                         store(k, j)

@@ -24,7 +24,11 @@ QUADRANTS = 4
 QUADRANT = P // QUADRANTS
 SCALE_ROWS = 4
 LOAD_AHEAD = 6
-PREP_AHEAD = 3
+Z_LEAD = 2
+HEAD_STEPS = 5
+TILES_A_STEP = 2
+JOINS_A_STEP = 2
+Z_LANES_A_STEP = 2
 GROUP = 2
 
 FLOPS = 2 * 2 * LANES * ROWS * FEAT * FEAT
@@ -74,9 +78,9 @@ def tile_blockresmlp_mixerblock_pa_t_e_kernel(
 
     with (
         tc.tile_pool(name="const", bufs=1) as const,
-        tc.tile_pool(name="rows_in", bufs=LOAD_AHEAD + 2) as rows_in,
+        tc.tile_pool(name="rows_in", bufs=LOAD_AHEAD + 4) as rows_in,
         tc.tile_pool(name="zpool", bufs=6) as zpool,
-        tc.tile_pool(name="work", bufs=4) as work,
+        tc.tile_pool(name="work", bufs=3) as work,
         tc.tile_pool(name="rows_out", bufs=4) as rows_out,
         tc.psum_pool(name="psum", bufs=2) as psum,
     ):
@@ -115,13 +119,17 @@ def tile_blockresmlp_mixerblock_pa_t_e_kernel(
         def rows_of(k):
             return BLOCKS[k] * P
 
+        def join_rows(k, part):
+            width = min(rows_of(k), 2 * P)
+            return slice(part * width, (part + 1) * width)
+
         def ts_of(k, bank):
             n = PACK // BLOCKS[k]
             return range(bank * n, (bank + 1) * n)
 
         def transpose_y(i):
             y_words = y_of[i][:].bitcast(F32)
-            zT = psum.tile([P, PACK, P], F32, bufs=1)
+            zT = psum.tile([P, PACK, P], F32, bufs=2)
             for t in range(PACK):
                 nc.tensor.transpose(zT[:, t, :], y_words[:, t:FEAT:PACK], identity[:])
             zT_of[i] = zT
@@ -137,21 +145,20 @@ def tile_blockresmlp_mixerblock_pa_t_e_kernel(
                 in_=zT_of[i][:].bitcast(BF16).rearrange("p t (b g) -> p g b t", g=LANES)[:, lanes],
             )
 
-        def quantise_z(k):
-            zq_of[k] = quantise(zg_of[k][:].rearrange("p g b t -> p (g b t)"), LANES * rows_of(k), "z")
+        def quantise_z(k, g):
+            zq_of[k, g] = quantise(zg_of[k][:, g, :, :].rearrange("p b t -> p (b t)"), rows_of(k), "z")
 
         def first_matmul(k, g, bank):
-            codes, plane = zq_of[k]
-            rows = slice(g * rows_of(k), (g + 1) * rows_of(k))
-            acc1 = psum.tile([P, PACK // BLOCKS[k], rows_of(k)], F32, bufs=3)
+            codes, plane = zq_of[k, g]
+            acc1 = psum.tile([P, PACK // BLOCKS[k], rows_of(k)], F32, bufs=2)
             for s, t in enumerate(ts_of(k, bank)):
                 cols = slice(t * P, (t + 1) * P)
                 nc.tensor.matmul_mx(
                     out=acc1[:, s, :],
                     lhsT=w1_codes[:, g, cols].bitcast(FP8X4),
                     lhsT_scale=w1_plane[:, g, cols],
-                    rhs=codes[:, rows].bitcast(FP8X4),
-                    rhs_scale=plane[:, rows],
+                    rhs=codes[:].bitcast(FP8X4),
+                    rhs_scale=plane[:],
                     start=True,
                     stop=True,
                 )
@@ -167,20 +174,32 @@ def tile_blockresmlp_mixerblock_pa_t_e_kernel(
                 for s, t in enumerate(ts_of(k, bank)):
                     nc.scalar.activation(out=part[:, t, :], in_=acc1[:, s, :], func=func, bias=b1_col[:, g, t : t + 1])
 
-        def elu_join(k, g):
-            hg = work.tile([P, rows_of(k), PACK], BF16, align_bytes=64)
+        def elu_join(k, g, part):
+            if part == 0:
+                hg = work.tile([P, rows_of(k), PACK], BF16, align_bytes=64)
+                hg_of[k, g] = hg
+            rows = join_rows(k, part)
             nc.vector.scalar_tensor_tensor(
-                out=hg[:],
-                in0=e_of[k, g][:].rearrange("p t b -> p b t"),
+                out=hg_of[k, g][:, rows, :],
+                in0=e_of[k, g][:, :, rows].rearrange("p t b -> p b t"),
                 scalar=-1.0,
-                in1=a_of[k, g][:].rearrange("p t b -> p b t"),
+                in1=a_of[k, g][:, :, rows].rearrange("p t b -> p b t"),
                 op0=ALU.add,
                 op1=ALU.min,
             )
-            hg_of[k, g] = hg
 
-        def quantise_h(k, g):
-            hq_of[k, g] = quantise(hg_of[k, g][:].rearrange("p b t -> p (b t)"), rows_of(k), "h")
+        def quantise_h(k, g, part):
+            if part == 0:
+                h_codes = work.tile([P, rows_of(k)], U32, align_bytes=64)
+                h_plane = work.tile([P, rows_of(k)], U8, align_bytes=64)
+                hq_of[k, g] = h_codes, h_plane
+            rows = join_rows(k, part)
+            codes, plane = hq_of[k, g]
+            nc.vector.quantize_mx(
+                out=codes[:, rows].bitcast(FP8X4),
+                scales=plane[:, rows],
+                in_=hg_of[k, g][:, rows, :].rearrange("p b t -> p (b t)"),
+            )
 
         def second_matmul(k, g, bank):
             codes, plane = hq_of[k, g]
@@ -200,7 +219,7 @@ def tile_blockresmlp_mixerblock_pa_t_e_kernel(
 
         def add_residual(k, g, bank):
             if (g, bank) == (0, 0):
-                r = work.tile([P, LANES, PACK, rows_of(k)], F32, bufs=2)
+                r = work.tile([P, LANES, PACK, rows_of(k)], F32)
                 r_of[k] = r
             for s, t in enumerate(ts_of(k, bank)):
                 nc.vector.scalar_tensor_tensor(
@@ -244,77 +263,100 @@ def tile_blockresmlp_mixerblock_pa_t_e_kernel(
         out_banks = [(k, j, pair) for k in blocks for pair in range(PAIRS) for j in range(BLOCKS[k])]
         steps = len(units)
         both = slice(0, LANES)
-        joined, quantised, added = [], {}, {}
-        n_first = n_second = n_out = n_copied = n_zq = 0
+        to_join = []
+        ready_h, added = {}, {}
+        n_first = n_second = n_out = n_copied = n_zq = n_split = 0
         n_tiles = 2
         n_loaded = LOAD_AHEAD
+        z_lanes = [(k, g) for k in blocks for g in range(LANES)]
 
         def parts(k, j, pair):
             n = PACK // BLOCKS[k]
             return {(k, g, t // n) for g in range(LANES) for t in range(pair * PAIRS, (pair + 1) * PAIRS)}
 
+        due = [2 * (FIRST[k] - Z_LEAD - (BLOCKS[k] - 1 - j)) for k in blocks for j in range(BLOCKS[k])]
+
+        def copy_banks(banks, scalar_share):
+            for n, (k, j, pair) in enumerate(banks):
+                copy_out(k, j, pair, scalar_copy if n in scalar_share else vector_copy)
+                if pair == 1:
+                    store(k, j)
+
         with tc.manual_schedule():
             transpose_y(0)
             split_lanes(0, both, scalar_copy)
             permute_columns(nc, w1_codes, w1_plane, raw1[0], raw1[1], 0)
-            quantise_z(0)
+            quantise_z(0, 0)
+            quantise_z(0, 1)
             permute_columns(nc, w1_codes, w1_plane, raw1[0], raw1[1], 1)
             transpose_y(1)
             split_lanes(1, both, vector_copy)
-            n_zq = 1
+            n_zq = LANES
+            n_split = 2
             step = 0
-            while n_out < len(out_banks):
-                draining = n_first >= steps
+            tiles, banks = [], []
+            while n_out < len(out_banks) or banks:
                 group = GROUP if 2 <= n_first < steps - 4 else 1
+                ending = n_first + group > steps - 4
                 take = units[n_first : n_first + group]
                 n_first += len(take)
-                prep = range(n_tiles, min(N_TILES, n_first // 2 + PREP_AHEAD))
-                n_tiles += len(prep)
-                for i in prep:
-                    if n_loaded < N_TILES:
-                        load_rows(n_loaded)
-                        n_loaded += 1
-                ending = n_first > steps - 4
-                seconds = [n for n in range(n_second, min(n_second + (GROUP if ending else group), steps)) if quantised.get(units[n][:2], step) < step]
+                for i in range(n_loaded, min(N_TILES, n_tiles + LOAD_AHEAD)):
+                    load_rows(i)
+                n_loaded = max(n_loaded, min(N_TILES, n_tiles + LOAD_AHEAD))
+                new_tiles = []
+                while n_tiles < N_TILES and len(new_tiles) < TILES_A_STEP and due[n_tiles] <= n_first:
+                    new_tiles.append(n_tiles)
+                    n_tiles += 1
+                most = GROUP if ending else group
+                seconds = [n for n in range(n_second, min(n_second + most, steps)) if ready_h.get(units[n][:2], step) < step]
                 n_second += len(seconds)
-                outs = []
+                new_banks = []
                 while (
                     n_out < len(out_banks)
-                    and len(outs) < (GROUP if ending else group)
+                    and len(new_banks) < most
                     and all(added.get(part, step) < step for part in parts(*out_banks[n_out]))
                 ):
-                    outs.append(out_banks[n_out])
+                    new_banks.append(out_banks[n_out])
                     n_out += 1
                 for unit in take:
                     first_matmul(*unit)
                 for n in seconds:
                     second_matmul(*units[n])
-                for bank in outs:
+                on_scalar = [n for n in range(len(banks)) if (n == 0 if n_first >= steps else (n_copied + n) % 8 in (0, 2, 5))]
+                n_copied += len(banks)
+                for i in tiles[-1:]:
+                    split_lanes(i, both, scalar_copy)
+                copy_banks(banks, on_scalar)
+                for unit in take:
+                    elu_parts(*unit)
+                for bank in new_banks:
                     transpose_out(*bank)
-                for i in prep:
+                for i in new_tiles[:-1]:
+                    transpose_y(i)
+                    split_lanes(i, both, vector_copy)
+                for i in new_tiles[-1:]:
                     transpose_y(i)
                 if step < LANES:
                     permute_columns(nc, w2_codes, w2_plane, raw2[0], raw2[1], step)
-                if n_zq < N_BLOCKS and FIRST[n_zq] + BLOCKS[n_zq] <= n_tiles - len(prep):
-                    quantise_z(n_zq)
-                    n_zq += 1
-                for k, g in joined:
-                    elu_join(k, g)
+                n_ready = n_split + (len(tiles) if step < HEAD_STEPS else 0)
+                for k, g in z_lanes[n_zq : n_zq + Z_LANES_A_STEP]:
+                    if FIRST[k] + BLOCKS[k] <= n_ready:
+                        quantise_z(k, g)
+                        n_zq += 1
+                n_split += len(tiles)
+                now = [part for part in to_join if part[3] < step][:JOINS_A_STEP]
+                for k, g, part, since in now:
+                    elu_join(k, g, part)
+                    to_join.remove((k, g, part, since))
                 for n in seconds:
                     add_residual(*units[n])
                     added[units[n]] = step
-                for k, g in joined:
-                    quantise_h(k, g)
-                    quantised[k, g] = step
-                joined = [unit[:2] for unit in take if unit[2] == BLOCKS[unit[0]] - 1]
-                for unit in take:
-                    elu_parts(*unit)
-                for i in prep:
-                    split_lanes(i, both, scalar_copy)
-                for n, (k, j, pair) in enumerate(outs):
-                    n_copied += 1
-                    on_scalar = (n == 0) if draining else n_copied % 8 in (0, 2, 5)
-                    copy_out(k, j, pair, scalar_copy if on_scalar else vector_copy)
-                    if pair == 1:
-                        store(k, j)
+                for k, g, part, since in now:
+                    quantise_h(k, g, part)
+                    if (part + 1) * 2 * P >= rows_of(k):
+                        ready_h[k, g] = step
+                for k, g, bank in take:
+                    if bank == BLOCKS[k] - 1:
+                        to_join.extend([(k, g, part, step) for part in range(max(1, BLOCKS[k] // 2))])
+                tiles, banks = new_tiles, new_banks
                 step += 1

@@ -15,16 +15,18 @@ PACK = 4
 LANES = 2
 ROWS = 4096
 FEAT = 512
-BLOCKS = [1] + [2] * 15 + [1]
+BLOCKS = [1, 1] + [2] * 15
 N_BLOCKS = len(BLOCKS)
 FIRST = [sum(BLOCKS[:k]) for k in range(N_BLOCKS)]
 N_TILES = ROWS // P
+HALVES = 2
+HALF = FEAT // HALVES
 PAIRS = PACK // 2
 QUADRANTS = 4
 QUADRANT = P // QUADRANTS
 SCALE_ROWS = 4
 LOAD_AHEAD = 6
-Z_LEAD = 2
+Z_LEAD = 3
 HEAD_STEPS = 5
 TILES_A_STEP = 2
 JOINS_A_STEP = 2
@@ -78,7 +80,7 @@ def tile_blockresmlp_mixerblock_pa_t_e_kernel(
 
     with (
         tc.tile_pool(name="const", bufs=1) as const,
-        tc.tile_pool(name="rows_in", bufs=LOAD_AHEAD + 4) as rows_in,
+        tc.tile_pool(name="rows_in", bufs=LOAD_AHEAD + 10) as rows_in,
         tc.tile_pool(name="zpool", bufs=6) as zpool,
         tc.tile_pool(name="work", bufs=3) as work,
         tc.tile_pool(name="rows_out", bufs=4) as rows_out,
@@ -101,6 +103,13 @@ def tile_blockresmlp_mixerblock_pa_t_e_kernel(
             load_rows(i)
         b1_col = load_bias(nc, const, b1, "b1")
         b2_col = load_bias(nc, const, b2, "b2")
+        b2_all = const.tile([P, LANES, FEAT], BF16)
+        nc.sync.dma_start(
+            out=b2_all[:].rearrange("p g d -> p (g d)"),
+            in_=b2.rearrange("g o d -> (g o d)").partition_broadcast(P),
+        )
+        b2_cols = const.tile([P, FEAT, LANES], BF16)
+        nc.gpsimd.tensor_copy(out=b2_cols[:], in_=b2_all[:].rearrange("p g d -> p d g"))
 
         w1_codes = const.tile([P, LANES, FEAT], U32, align_bytes=64)
         w1_plane = const.tile([P, LANES, FEAT], U8, align_bytes=64)
@@ -166,8 +175,8 @@ def tile_blockresmlp_mixerblock_pa_t_e_kernel(
 
         def elu_parts(k, g, bank):
             if bank == 0:
-                e = work.tile([P, PACK, rows_of(k)], F32)
-                a = work.tile([P, PACK, rows_of(k)], BF16)
+                e = work.tile([P, PACK, rows_of(k)], F32, bufs=4)
+                a = work.tile([P, PACK, rows_of(k)], BF16, bufs=4)
                 e_of[k, g], a_of[k, g] = e, a
             acc1 = acc1_of[k, g, bank]
             for func, part in ((ACT.Exp, e_of[k, g]), (ACT.Relu, a_of[k, g])):
@@ -175,12 +184,12 @@ def tile_blockresmlp_mixerblock_pa_t_e_kernel(
                     nc.scalar.activation(out=part[:, t, :], in_=acc1[:, s, :], func=func, bias=b1_col[:, g, t : t + 1])
 
         def elu_join(k, g, part):
-            if part == 0:
-                hg = work.tile([P, rows_of(k), PACK], BF16, align_bytes=64)
-                hg_of[k, g] = hg
+            if g == 0:
+                hg = work.tile([P, LANES, rows_of(k), PACK], BF16, bufs=5, align_bytes=64)
+                hg_of[k] = hg
             rows = join_rows(k, part)
             nc.vector.scalar_tensor_tensor(
-                out=hg_of[k, g][:, rows, :],
+                out=hg_of[k][:, g, rows, :],
                 in0=e_of[k, g][:, :, rows].rearrange("p t b -> p b t"),
                 scalar=-1.0,
                 in1=a_of[k, g][:, :, rows].rearrange("p t b -> p b t"),
@@ -198,12 +207,12 @@ def tile_blockresmlp_mixerblock_pa_t_e_kernel(
             nc.vector.quantize_mx(
                 out=codes[:, rows].bitcast(FP8X4),
                 scales=plane[:, rows],
-                in_=hg_of[k, g][:, rows, :].rearrange("p b t -> p (b t)"),
+                in_=hg_of[k][:, g, rows, :].rearrange("p b t -> p (b t)"),
             )
 
         def second_matmul(k, g, bank):
             codes, plane = hq_of[k, g]
-            acc2 = psum.tile([P, PACK // BLOCKS[k], rows_of(k)], F32)
+            acc2 = psum.tile([P, PACK // BLOCKS[k], rows_of(k)], F32, bufs=3)
             for s, t in enumerate(ts_of(k, bank)):
                 cols = slice(t * P, (t + 1) * P)
                 nc.tensor.matmul_mx(
@@ -216,6 +225,47 @@ def tile_blockresmlp_mixerblock_pa_t_e_kernel(
                     stop=True,
                 )
             acc2_of[k, g, bank] = acc2
+
+        def second_matmul_direct(k, j, half):
+            feats = slice(half * HALF, (half + 1) * HALF)
+            rows = slice(j * P, (j + 1) * P)
+            acc2 = psum.tile([P, LANES, HALF], F32, bufs=3)
+            for g in range(LANES):
+                codes, plane = hq_of[k, g]
+                nc.tensor.matmul_mx(
+                    out=acc2[:, g, :],
+                    lhsT=codes[:, rows].bitcast(FP8X4),
+                    lhsT_scale=plane[:, rows],
+                    rhs=raw2[0][:, g, feats].bitcast(FP8X4),
+                    rhs_scale=raw2[1][:, g, feats],
+                    start=True,
+                    stop=True,
+                )
+            acc2_of[k, j, half] = acc2
+
+        def residual_and_bias(k, j, last):
+            if BLOCKS[last] == 2:
+                o_sb = hg_of[last][:].rearrange("p g b t -> p (g b t)").bitcast(F32)
+            else:
+                o_new = rows_out.tile([P, LANES * FEAT], F32)
+                o_sb = o_new[:]
+            o_of[k, j] = o_sb
+            nc.gpsimd.tensor_tensor(
+                out=o_sb,
+                in0=y_of[FIRST[k] + j][:],
+                in1=b2_cols[:].rearrange("p d g -> p (d g)"),
+                op=ALU.add,
+            )
+
+        def add_direct(k, j, half):
+            width = LANES * HALF
+            o_cols = o_of[k, j][:, half * width : (half + 1) * width].rearrange("p (d g) -> p d g", g=LANES)
+            nc.vector.tensor_tensor(
+                out=o_cols, in0=acc2_of[k, j, half][:].rearrange("p g d -> p d g"), in1=o_cols, op=ALU.add
+            )
+            if half == 1:
+                i = FIRST[k] + j
+                nc.sync.dma_start(out=out[i * P : (i + 1) * P, :], in_=o_of[k, j])
 
         def add_residual(k, g, bank):
             if (g, bank) == (0, 0):
@@ -232,7 +282,7 @@ def tile_blockresmlp_mixerblock_pa_t_e_kernel(
                 )
 
         def transpose_out(k, j, pair):
-            oT = psum.tile([P, PAIRS, LANES, P], F32)
+            oT = psum.tile([P, PAIRS, LANES, P], F32, bufs=1)
             for s in range(PAIRS):
                 for g in range(LANES):
                     nc.tensor.transpose(
@@ -260,7 +310,19 @@ def tile_blockresmlp_mixerblock_pa_t_e_kernel(
         blocks = range(N_BLOCKS)
         block_of = [k for k in blocks for j in range(BLOCKS[k])]
         units = [(k, g, bank) for k in blocks for g in range(LANES) for bank in range(BLOCKS[k])]
-        out_banks = [(k, j, pair) for k in blocks for pair in range(PAIRS) for j in range(BLOCKS[k])]
+        direct = [k % 2 == 0 for k in blocks]
+        second_units = [
+            (k, j, half)
+            for k in blocks
+            for j, half in (
+                [(j, half) for j in range(BLOCKS[k]) for half in range(HALVES)]
+                if direct[k]
+                else [(g, bank) for g in range(LANES) for bank in range(BLOCKS[k])]
+            )
+        ]
+        out_banks = [
+            (k, j, pair) for k in blocks if not direct[k] for pair in range(PAIRS) for j in range(BLOCKS[k])
+        ]
         steps = len(units)
         both = slice(0, LANES)
         to_join = []
@@ -294,9 +356,9 @@ def tile_blockresmlp_mixerblock_pa_t_e_kernel(
             n_zq = LANES
             n_split = 2
             step = 0
-            tiles, banks = [], []
-            while n_out < len(out_banks) or banks:
-                group = GROUP if 2 <= n_first < steps - 4 else 1
+            tiles, banks, summed = [], [], []
+            while n_second < steps or n_out < len(out_banks) or banks or summed:
+                group = GROUP if n_first < steps - 4 else 1
                 ending = n_first + group > steps - 4
                 take = units[n_first : n_first + group]
                 n_first += len(take)
@@ -308,27 +370,58 @@ def tile_blockresmlp_mixerblock_pa_t_e_kernel(
                     new_tiles.append(n_tiles)
                     n_tiles += 1
                 most = GROUP if ending else group
-                seconds = [n for n in range(n_second, min(n_second + most, steps)) if ready_h.get(units[n][:2], step) < step]
+                seconds = []
+                for k, j, half in second_units[n_second : n_second + most]:
+                    needs = [(k, g) for g in range(LANES)] if direct[k] else [(k, j)]
+                    if all(ready_h.get(lane, step) < step for lane in needs):
+                        seconds.append((k, j, half))
                 n_second += len(seconds)
                 new_banks = []
                 while (
                     n_out < len(out_banks)
-                    and len(new_banks) < most
+                    and len(new_banks) < (GROUP if ending else 1)
                     and all(added.get(part, step) < step for part in parts(*out_banks[n_out]))
                 ):
                     new_banks.append(out_banks[n_out])
                     n_out += 1
+                short = step < HEAD_STEPS or ending
+                joining, adding = short or step % 2 == 0, short or step % 2 == 1
                 for unit in take:
                     first_matmul(*unit)
-                for n in seconds:
-                    second_matmul(*units[n])
-                on_scalar = [n for n in range(len(banks)) if (n == 0 if n_first >= steps else (n_copied + n) % 8 in (0, 2, 5))]
-                n_copied += len(banks)
+                for unit in seconds:
+                    (second_matmul_direct if direct[unit[0]] else second_matmul)(*unit)
+                summed = summed + seconds
+                on_scalar = [n for n in range(len(banks)) if (n_first >= steps - 8 or step % 2 == 0)]
                 for i in tiles[-1:]:
                     split_lanes(i, both, scalar_copy)
                 copy_banks(banks, on_scalar)
                 for unit in take:
                     elu_parts(*unit)
+                now = [part for part in to_join if part[3] < step][:JOINS_A_STEP] if joining else []
+                for k, g, part, since in now:
+                    elu_join(k, g, part)
+                    to_join.remove((k, g, part, since))
+                if step < LANES:
+                    permute_columns(nc, w2_codes, w2_plane, raw2[0], raw2[1], step)
+                n_ready = n_split + (len(tiles) if step < HEAD_STEPS else 0)
+                for k, g in z_lanes[n_zq : n_zq + Z_LANES_A_STEP] if joining else []:
+                    if FIRST[k] + BLOCKS[k] <= n_ready:
+                        quantise_z(k, g)
+                        n_zq += 1
+                n_split += len(tiles)
+                for k, g, part, since in now:
+                    quantise_h(k, g, part)
+                    if (part + 1) * 2 * P >= rows_of(k):
+                        ready_h[k, g] = step
+                        if g == 1:
+                            for kk, j in ((k, BLOCKS[k] - 1), (k + 1, 0)):
+                                if kk < N_BLOCKS and direct[kk] and (kk, j) not in o_of:
+                                    residual_and_bias(kk, j, k)
+                if adding:
+                    for unit in summed:
+                        (add_direct if direct[unit[0]] else add_residual)(*unit)
+                        added[unit] = step
+                    summed = []
                 for bank in new_banks:
                     transpose_out(*bank)
                 for i in new_tiles[:-1]:
@@ -336,25 +429,6 @@ def tile_blockresmlp_mixerblock_pa_t_e_kernel(
                     split_lanes(i, both, vector_copy)
                 for i in new_tiles[-1:]:
                     transpose_y(i)
-                if step < LANES:
-                    permute_columns(nc, w2_codes, w2_plane, raw2[0], raw2[1], step)
-                n_ready = n_split + (len(tiles) if step < HEAD_STEPS else 0)
-                for k, g in z_lanes[n_zq : n_zq + Z_LANES_A_STEP]:
-                    if FIRST[k] + BLOCKS[k] <= n_ready:
-                        quantise_z(k, g)
-                        n_zq += 1
-                n_split += len(tiles)
-                now = [part for part in to_join if part[3] < step][:JOINS_A_STEP]
-                for k, g, part, since in now:
-                    elu_join(k, g, part)
-                    to_join.remove((k, g, part, since))
-                for n in seconds:
-                    add_residual(*units[n])
-                    added[units[n]] = step
-                for k, g, part, since in now:
-                    quantise_h(k, g, part)
-                    if (part + 1) * 2 * P >= rows_of(k):
-                        ready_h[k, g] = step
                 for k, g, bank in take:
                     if bank == BLOCKS[k] - 1:
                         to_join.extend([(k, g, part, step) for part in range(max(1, BLOCKS[k] // 2))])

@@ -109,7 +109,6 @@ def tile_blockresmlp_mixerblock_pa_t_e_kernel(
             in_=b2.rearrange("g o d -> (g o d)").partition_broadcast(P),
         )
         b2_cols = const.tile([P, FEAT, LANES], BF16)
-        nc.gpsimd.tensor_copy(out=b2_cols[:], in_=b2_all[:].rearrange("p g d -> p d g"))
 
         w1_codes = const.tile([P, LANES, FEAT], U32, align_bytes=64)
         w1_plane = const.tile([P, LANES, FEAT], U8, align_bytes=64)
@@ -244,7 +243,7 @@ def tile_blockresmlp_mixerblock_pa_t_e_kernel(
             acc2_of[k, j, half] = acc2
 
         def residual_and_bias(k, j, last):
-            if BLOCKS[last] == 2:
+            if last is not None and BLOCKS[last] == 2:
                 o_sb = hg_of[last][:].rearrange("p g b t -> p (g b t)").bitcast(F32)
             else:
                 o_new = rows_out.tile([P, LANES * FEAT], F32)
@@ -310,7 +309,7 @@ def tile_blockresmlp_mixerblock_pa_t_e_kernel(
         blocks = range(N_BLOCKS)
         block_of = [k for k in blocks for j in range(BLOCKS[k])]
         units = [(k, g, bank) for k in blocks for g in range(LANES) for bank in range(BLOCKS[k])]
-        direct = [k % 2 == 0 for k in blocks]
+        direct = [k % 2 == 0 and k > 0 for k in blocks]
         second_units = [
             (k, j, half)
             for k in blocks
@@ -379,7 +378,7 @@ def tile_blockresmlp_mixerblock_pa_t_e_kernel(
                 new_banks = []
                 while (
                     n_out < len(out_banks)
-                    and len(new_banks) < (GROUP if ending else 1)
+                    and len(new_banks) < (GROUP if n_second >= steps else 1)
                     and all(added.get(part, step) < step for part in parts(*out_banks[n_out]))
                 ):
                     new_banks.append(out_banks[n_out])
@@ -401,6 +400,8 @@ def tile_blockresmlp_mixerblock_pa_t_e_kernel(
                 for k, g, part, since in now:
                     elu_join(k, g, part)
                     to_join.remove((k, g, part, since))
+                if step == 1:
+                    nc.vector.tensor_copy(out=b2_cols[:], in_=b2_all[:].rearrange("p g d -> p d g"))
                 if step < LANES:
                     permute_columns(nc, w2_codes, w2_plane, raw2[0], raw2[1], step)
                 n_ready = n_split + (len(tiles) if step < HEAD_STEPS else 0)
@@ -413,10 +414,10 @@ def tile_blockresmlp_mixerblock_pa_t_e_kernel(
                     quantise_h(k, g, part)
                     if (part + 1) * 2 * P >= rows_of(k):
                         ready_h[k, g] = step
-                        if g == 1:
+                        if g == 1 or k == N_BLOCKS - 1:
                             for kk, j in ((k, BLOCKS[k] - 1), (k + 1, 0)):
                                 if kk < N_BLOCKS and direct[kk] and (kk, j) not in o_of:
-                                    residual_and_bias(kk, j, k)
+                                    residual_and_bias(kk, j, k if g == 1 else None)
                 if adding:
                     for unit in summed:
                         (add_direct if direct[unit[0]] else add_residual)(*unit)

import concourse.mybir as mybir
from concourse.masks import make_identity

F32 = mybir.dt.float32
BF16 = mybir.dt.bfloat16
I32 = mybir.dt.int32
U32 = mybir.dt.uint32
U8 = mybir.dt.uint8
FP8X4 = mybir.dt.float8_e4m3fn_x4
ACT = mybir.ActivationFunctionType
ALU = mybir.AluOpType

P = 128
PACK = 4
LANES = 2
ROWS = 4096
FEAT = 512
BLOCKS = [1, 1] + [2] * 15
N_BLOCKS = len(BLOCKS)
FIRST = [sum(BLOCKS[:k]) for k in range(N_BLOCKS)]
N_TILES = ROWS // P
HALVES = 2
HALF = FEAT // HALVES
PAIRS = PACK // 2
QUADRANTS = 4
QUADRANT = P // QUADRANTS
SCALE_ROWS = 4
LOAD_AHEAD = 6
Z_LEAD = 3
HEAD_STEPS = 5
TILES_A_STEP = 2
JOINS_A_STEP = 2
Z_LANES_A_STEP = 2
GROUP = 2

FLOPS = 2 * 2 * LANES * ROWS * FEAT * FEAT


def load_weight(nc, pool, words, scales, label):
    codes = pool.tile([P, LANES, FEAT], U32, name=label + "_raw_codes", align_bytes=64)
    plane = pool.tile([P, LANES, FEAT], U8, name=label + "_raw_plane", align_bytes=64)
    nc.gpsimd.memset(plane[:].bitcast(I32), 0)
    nc.sync.dma_start(
        out=codes[:].bitcast(I32),
        in_=words.rearrange("g p n t -> p g (n t)").bitcast(I32),
    )
    for quadrant in range(QUADRANTS):
        first = QUADRANT * quadrant
        q_rows = slice(SCALE_ROWS * quadrant, SCALE_ROWS * (quadrant + 1))
        nc.sync.dma_start(
            out=plane[first : first + SCALE_ROWS, :, :].bitcast(I32),
            in_=scales[:, q_rows, :].bitcast(I32).rearrange("g r n -> r g n"),
        )
    return codes, plane


def permute_columns(nc, codes, plane, raw_codes, raw_plane, g):
    nc.vector.tensor_copy(
        out=codes[:, g, :].bitcast(I32).rearrange("p (t m) -> p t m", t=PACK),
        in_=raw_codes[:, g, :].bitcast(I32).rearrange("p (m t) -> p t m", t=PACK),
    )
    nc.vector.tensor_copy(
        out=plane[:, g, :].rearrange("p (t m) -> p t m", t=PACK),
        in_=raw_plane[:, g, :].rearrange("p (m t) -> p t m", t=PACK),
    )


def load_bias(nc, pool, bias, label):
    raw = pool.tile([P, LANES, PACK], BF16, name=label + "_raw")
    nc.scalar.dma_start(out=raw[:], in_=bias.rearrange("g o (p t) -> p (g o) t", t=PACK))
    column = pool.tile([P, LANES, PACK], F32, name=label + "_column")
    nc.vector.tensor_copy(out=column[:], in_=raw[:])
    return column


def tile_blockresmlp_mixerblock_pa_t_e_kernel(
    tc, y_lanes, w1_words, w1_scales, b1, w2_words, w2_scales, b2, out
):
    nc = tc.nc

    with (
        tc.tile_pool(name="const", bufs=1) as const,
        tc.tile_pool(name="rows_in", bufs=LOAD_AHEAD + 10) as rows_in,
        tc.tile_pool(name="zpool", bufs=6) as zpool,
        tc.tile_pool(name="work", bufs=3) as work,
        tc.tile_pool(name="rows_out", bufs=4) as rows_out,
        tc.psum_pool(name="psum", bufs=2) as psum,
    ):
        y_of, zT_of, zg_of, zq_of, acc1_of, e_of, a_of = {}, {}, {}, {}, {}, {}, {}
        hg_of, hq_of, acc2_of, r_of, oT_of, o_of = {}, {}, {}, {}, {}, {}

        def load_rows(i):
            y_sb = rows_in.tile([P, LANES * FEAT], BF16)
            nc.sync.dma_start(out=y_sb[:], in_=y_lanes[i * P : (i + 1) * P, :])
            y_of[i] = y_sb

        load_rows(0)
        raw1 = load_weight(nc, const, w1_words, w1_scales, "w1")
        for i in range(1, 3):
            load_rows(i)
        raw2 = load_weight(nc, const, w2_words, w2_scales, "w2")
        for i in range(3, LOAD_AHEAD):
            load_rows(i)
        b1_col = load_bias(nc, const, b1, "b1")
        b2_col = load_bias(nc, const, b2, "b2")
        b2_all = const.tile([P, LANES, FEAT], BF16)
        nc.sync.dma_start(
            out=b2_all[:].rearrange("p g d -> p (g d)"),
            in_=b2.rearrange("g o d -> (g o d)").partition_broadcast(P),
        )
        b2_cols = const.tile([P, FEAT, LANES], BF16)

        w1_codes = const.tile([P, LANES, FEAT], U32, align_bytes=64)
        w1_plane = const.tile([P, LANES, FEAT], U8, align_bytes=64)
        w2_codes = const.tile([P, LANES, FEAT], U32, align_bytes=64)
        w2_plane = const.tile([P, LANES, FEAT], U8, align_bytes=64)

        identity = const.tile([P, P], F32)
        make_identity(nc, identity[:])

        def quantise(grouped, width, label):
            codes = work.tile([P, width], U32, name=label + "_codes", align_bytes=64)
            plane = work.tile([P, width], U8, name=label + "_plane", align_bytes=64)
            nc.vector.quantize_mx(out=codes[:].bitcast(FP8X4), scales=plane[:], in_=grouped)
            return codes, plane

        def rows_of(k):
            return BLOCKS[k] * P

        def join_rows(k, part):
            width = min(rows_of(k), 2 * P)
            return slice(part * width, (part + 1) * width)

        def ts_of(k, bank):
            n = PACK // BLOCKS[k]
            return range(bank * n, (bank + 1) * n)

        def transpose_y(i):
            y_words = y_of[i][:].bitcast(F32)
            zT = psum.tile([P, PACK, P], F32, bufs=2)
            for t in range(PACK):
                nc.tensor.transpose(zT[:, t, :], y_words[:, t:FEAT:PACK], identity[:])
            zT_of[i] = zT

        def split_lanes(i, lanes, copy):
            k = block_of[i]
            j = i - FIRST[k]
            if k not in zg_of:
                zg = zpool.tile([P, LANES, rows_of(k), PACK], BF16, align_bytes=64)
                zg_of[k] = zg
            copy(
                out=zg_of[k][:, lanes, j * P : (j + 1) * P, :],
                in_=zT_of[i][:].bitcast(BF16).rearrange("p t (b g) -> p g b t", g=LANES)[:, lanes],
            )

        def quantise_z(k, g):
            zq_of[k, g] = quantise(zg_of[k][:, g, :, :].rearrange("p b t -> p (b t)"), rows_of(k), "z")

        def first_matmul(k, g, bank):
            codes, plane = zq_of[k, g]
            acc1 = psum.tile([P, PACK // BLOCKS[k], rows_of(k)], F32, bufs=2)
            for s, t in enumerate(ts_of(k, bank)):
                cols = slice(t * P, (t + 1) * P)
                nc.tensor.matmul_mx(
                    out=acc1[:, s, :],
                    lhsT=w1_codes[:, g, cols].bitcast(FP8X4),
                    lhsT_scale=w1_plane[:, g, cols],
                    rhs=codes[:].bitcast(FP8X4),
                    rhs_scale=plane[:],
                    start=True,
                    stop=True,
                )
            acc1_of[k, g, bank] = acc1

        def elu_parts(k, g, bank):
            if bank == 0:
                e = work.tile([P, PACK, rows_of(k)], F32, bufs=4)
                a = work.tile([P, PACK, rows_of(k)], BF16, bufs=4)
                e_of[k, g], a_of[k, g] = e, a
            acc1 = acc1_of[k, g, bank]
            for func, part in ((ACT.Exp, e_of[k, g]), (ACT.Relu, a_of[k, g])):
                for s, t in enumerate(ts_of(k, bank)):
                    nc.scalar.activation(out=part[:, t, :], in_=acc1[:, s, :], func=func, bias=b1_col[:, g, t : t + 1])

        def elu_join(k, g, part):
            if g == 0:
                hg = work.tile([P, LANES, rows_of(k), PACK], BF16, bufs=5, align_bytes=64)
                hg_of[k] = hg
            rows = join_rows(k, part)
            nc.vector.scalar_tensor_tensor(
                out=hg_of[k][:, g, rows, :],
                in0=e_of[k, g][:, :, rows].rearrange("p t b -> p b t"),
                scalar=-1.0,
                in1=a_of[k, g][:, :, rows].rearrange("p t b -> p b t"),
                op0=ALU.add,
                op1=ALU.min,
            )

        def quantise_h(k, g, part):
            if part == 0:
                h_codes = work.tile([P, rows_of(k)], U32, align_bytes=64)
                h_plane = work.tile([P, rows_of(k)], U8, align_bytes=64)
                hq_of[k, g] = h_codes, h_plane
            rows = join_rows(k, part)
            codes, plane = hq_of[k, g]
            nc.vector.quantize_mx(
                out=codes[:, rows].bitcast(FP8X4),
                scales=plane[:, rows],
                in_=hg_of[k][:, g, rows, :].rearrange("p b t -> p (b t)"),
            )

        def second_matmul(k, g, bank):
            codes, plane = hq_of[k, g]
            acc2 = psum.tile([P, PACK // BLOCKS[k], rows_of(k)], F32, bufs=3)
            for s, t in enumerate(ts_of(k, bank)):
                cols = slice(t * P, (t + 1) * P)
                nc.tensor.matmul_mx(
                    out=acc2[:, s, :],
                    lhsT=w2_codes[:, g, cols].bitcast(FP8X4),
                    lhsT_scale=w2_plane[:, g, cols],
                    rhs=codes[:].bitcast(FP8X4),
                    rhs_scale=plane[:],
                    start=True,
                    stop=True,
                )
            acc2_of[k, g, bank] = acc2

        def second_matmul_direct(k, j, half):
            feats = slice(half * HALF, (half + 1) * HALF)
            rows = slice(j * P, (j + 1) * P)
            acc2 = psum.tile([P, LANES, HALF], F32, bufs=3)
            for g in range(LANES):
                codes, plane = hq_of[k, g]
                nc.tensor.matmul_mx(
                    out=acc2[:, g, :],
                    lhsT=codes[:, rows].bitcast(FP8X4),
                    lhsT_scale=plane[:, rows],
                    rhs=raw2[0][:, g, feats].bitcast(FP8X4),
                    rhs_scale=raw2[1][:, g, feats],
                    start=True,
                    stop=True,
                )
            acc2_of[k, j, half] = acc2

        def residual_and_bias(k, j, last):
            if last is not None and BLOCKS[last] == 2:
                o_sb = hg_of[last][:].rearrange("p g b t -> p (g b t)").bitcast(F32)
            else:
                o_new = rows_out.tile([P, LANES * FEAT], F32)
                o_sb = o_new[:]
            o_of[k, j] = o_sb
            nc.gpsimd.tensor_tensor(
                out=o_sb,
                in0=y_of[FIRST[k] + j][:],
                in1=b2_cols[:].rearrange("p d g -> p (d g)"),
                op=ALU.add,
            )

        def add_direct(k, j, half):
            width = LANES * HALF
            o_cols = o_of[k, j][:, half * width : (half + 1) * width].rearrange("p (d g) -> p d g", g=LANES)
            nc.vector.tensor_tensor(
                out=o_cols, in0=acc2_of[k, j, half][:].rearrange("p g d -> p d g"), in1=o_cols, op=ALU.add
            )
            if half == 1:
                i = FIRST[k] + j
                nc.sync.dma_start(out=out[i * P : (i + 1) * P, :], in_=o_of[k, j])

        def add_residual(k, g, bank):
            if (g, bank) == (0, 0):
                r = work.tile([P, LANES, PACK, rows_of(k)], F32)
                r_of[k] = r
            for s, t in enumerate(ts_of(k, bank)):
                nc.vector.scalar_tensor_tensor(
                    out=r_of[k][:, g, t, :],
                    in0=acc2_of[k, g, bank][:, s, :],
                    scalar=b2_col[:, g, t : t + 1],
                    in1=zg_of[k][:, g, :, t],
                    op0=ALU.add,
                    op1=ALU.add,
                )

        def transpose_out(k, j, pair):
            oT = psum.tile([P, PAIRS, LANES, P], F32, bufs=1)
            for s in range(PAIRS):
                for g in range(LANES):
                    nc.tensor.transpose(
                        oT[:, s, g, :], r_of[k][:, g, pair * PAIRS + s, j * P : (j + 1) * P], identity[:]
                    )
            oT_of[k, j, pair] = oT

        def copy_out(k, j, pair, copy):
            if (k, j) not in o_of:
                o_sb = rows_out.tile([P, P, PAIRS, PAIRS * LANES], F32)
                o_of[k, j] = o_sb
            copy(
                out=o_of[k, j][:, :, pair, :],
                in_=oT_of[k, j, pair][:].rearrange("b s g p -> b p (s g)"),
            )

        def store(k, j):
            i = FIRST[k] + j
            nc.sync.dma_start(
                out=out[i * P : (i + 1) * P, :], in_=o_of[k, j][:].rearrange("b p u c -> b (p u c)")
            )

        scalar_copy, vector_copy = nc.scalar.copy, nc.vector.tensor_copy

        blocks = range(N_BLOCKS)
        block_of = [k for k in blocks for j in range(BLOCKS[k])]
        units = [(k, g, bank) for k in blocks for g in range(LANES) for bank in range(BLOCKS[k])]
        direct = [k % 2 == 0 and k > 0 for k in blocks]
        second_units = [
            (k, j, half)
            for k in blocks
            for j, half in (
                [(j, half) for j in range(BLOCKS[k]) for half in range(HALVES)]
                if direct[k]
                else [(g, bank) for g in range(LANES) for bank in range(BLOCKS[k])]
            )
        ]
        out_banks = [
            (k, j, pair) for k in blocks if not direct[k] for pair in range(PAIRS) for j in range(BLOCKS[k])
        ]
        steps = len(units)
        both = slice(0, LANES)
        to_join = []
        ready_h, added = {}, {}
        n_first = n_second = n_out = n_copied = n_zq = n_split = 0
        n_tiles = 2
        n_loaded = LOAD_AHEAD
        z_lanes = [(k, g) for k in blocks for g in range(LANES)]

        def parts(k, j, pair):
            n = PACK // BLOCKS[k]
            return {(k, g, t // n) for g in range(LANES) for t in range(pair * PAIRS, (pair + 1) * PAIRS)}

        due = [2 * (FIRST[k] - Z_LEAD - (BLOCKS[k] - 1 - j)) for k in blocks for j in range(BLOCKS[k])]

        def copy_banks(banks, scalar_share):
            for n, (k, j, pair) in enumerate(banks):
                copy_out(k, j, pair, scalar_copy if n in scalar_share else vector_copy)
                if pair == 1:
                    store(k, j)

        with tc.manual_schedule():
            transpose_y(0)
            split_lanes(0, both, scalar_copy)
            permute_columns(nc, w1_codes, w1_plane, raw1[0], raw1[1], 0)
            quantise_z(0, 0)
            quantise_z(0, 1)
            permute_columns(nc, w1_codes, w1_plane, raw1[0], raw1[1], 1)
            transpose_y(1)
            split_lanes(1, both, vector_copy)
            n_zq = LANES
            n_split = 2
            step = 0
            tiles, banks, summed = [], [], []
            while n_second < steps or n_out < len(out_banks) or banks or summed:
                group = GROUP if n_first < steps - 4 else 1
                ending = n_first + group > steps - 4
                take = units[n_first : n_first + group]
                n_first += len(take)
                for i in range(n_loaded, min(N_TILES, n_tiles + LOAD_AHEAD)):
                    load_rows(i)
                n_loaded = max(n_loaded, min(N_TILES, n_tiles + LOAD_AHEAD))
                new_tiles = []
                while n_tiles < N_TILES and len(new_tiles) < TILES_A_STEP and due[n_tiles] <= n_first:
                    new_tiles.append(n_tiles)
                    n_tiles += 1
                most = GROUP if ending else group
                seconds = []
                for k, j, half in second_units[n_second : n_second + most]:
                    needs = [(k, g) for g in range(LANES)] if direct[k] else [(k, j)]
                    if all(ready_h.get(lane, step) < step for lane in needs):
                        seconds.append((k, j, half))
                n_second += len(seconds)
                new_banks = []
                while (
                    n_out < len(out_banks)
                    and len(new_banks) < (GROUP if n_second >= steps else 1)
                    and all(added.get(part, step) < step for part in parts(*out_banks[n_out]))
                ):
                    new_banks.append(out_banks[n_out])
                    n_out += 1
                short = step < HEAD_STEPS or ending
                joining, adding = short or step % 2 == 0, short or step % 2 == 1
                for unit in take:
                    first_matmul(*unit)
                for unit in seconds:
                    (second_matmul_direct if direct[unit[0]] else second_matmul)(*unit)
                summed = summed + seconds
                on_scalar = [n for n in range(len(banks)) if (n_first >= steps - 8 or step % 2 == 0)]
                for i in tiles[-1:]:
                    split_lanes(i, both, scalar_copy)
                copy_banks(banks, on_scalar)
                for unit in take:
                    elu_parts(*unit)
                now = [part for part in to_join if part[3] < step][:JOINS_A_STEP] if joining else []
                for k, g, part, since in now:
                    elu_join(k, g, part)
                    to_join.remove((k, g, part, since))
                if step == 1:
                    nc.vector.tensor_copy(out=b2_cols[:], in_=b2_all[:].rearrange("p g d -> p d g"))
                if step < LANES:
                    permute_columns(nc, w2_codes, w2_plane, raw2[0], raw2[1], step)
                n_ready = n_split + (len(tiles) if step < HEAD_STEPS else 0)
                for k, g in z_lanes[n_zq : n_zq + Z_LANES_A_STEP] if joining else []:
                    if FIRST[k] + BLOCKS[k] <= n_ready:
                        quantise_z(k, g)
                        n_zq += 1
                n_split += len(tiles)
                for k, g, part, since in now:
                    quantise_h(k, g, part)
                    if (part + 1) * 2 * P >= rows_of(k):
                        ready_h[k, g] = step
                        if g == 1 or k == N_BLOCKS - 1:
                            for kk, j in ((k, BLOCKS[k] - 1), (k + 1, 0)):
                                if kk < N_BLOCKS and direct[kk] and (kk, j) not in o_of:
                                    residual_and_bias(kk, j, k if g == 1 else None)
                if adding:
                    for unit in summed:
                        (add_direct if direct[unit[0]] else add_residual)(*unit)
                        added[unit] = step
                    summed = []
                for bank in new_banks:
                    transpose_out(*bank)
                for i in new_tiles[:-1]:
                    transpose_y(i)
                    split_lanes(i, both, vector_copy)
                for i in new_tiles[-1:]:
                    transpose_y(i)
                for k, g, bank in take:
                    if bank == BLOCKS[k] - 1:
                        to_join.extend([(k, g, part, step) for part in range(max(1, BLOCKS[k] // 2))])
                tiles, banks = new_tiles, new_banks
                step += 1
